import numpy as np
import ml_dtypes


def mxq(x, axis, fmt="e4m3"):
    dtype, down = {"e4m3": (ml_dtypes.float8_e4m3fn, 7), "e5m2": (ml_dtypes.float8_e5m2, 14)}[fmt]
    v = np.moveaxis(np.asarray(x, np.float32).astype(ml_dtypes.bfloat16).astype(np.float64), axis, -1)
    blocks = v.reshape(v.shape[:-1] + (-1, 32))
    amax = np.abs(blocks).max(-1, keepdims=True)
    byte = np.maximum(np.where(amax > 0, np.frexp(amax)[1] - 1 + 127, 0) - down, 1)
    scale = np.exp2(byte - 127.0)
    codes = (blocks / scale).astype(np.float32).astype(dtype).astype(np.float64)
    return np.moveaxis((codes * scale).reshape(v.shape), -1, axis)


WIDE = False


def mx_kscale(k):
    if not WIDE:
        return np.ones(k)
    levels = np.array([10, -10, 5, -5, 0])
    a = np.random.permutation(np.resize(levels, k // 512 * 4)).reshape(k // 512, 4)
    idx = np.arange(k)
    return np.exp2(a[idx // 512, idx % 128 // 32])


BF16 = ml_dtypes.bfloat16


def bf(x):
    return np.asarray(x, np.float32).astype(BF16)


def f64(x):
    return np.asarray(x).astype(np.float64)


E2M1 = np.array([0.0, 0.5, 1.0, 1.5, 2.0, 3.0, 4.0, 6.0, -0.0, -0.5, -1.0, -1.5, -2.0, -3.0, -4.0, -6.0])


def pack_weight(w, fmt):
    k, n = w.shape
    w = f64(bf(w)).reshape(k // 32, 32, n)
    amax = np.abs(w).max(1)
    if fmt == "e4m3":
        byte = np.frexp(amax)[1] - 1 + 127 - 7
    else:
        mant, ex = np.frexp(amax / 6.0)
        byte = np.where(mant > 0.5, ex, ex - 1) + 127
    byte = np.clip(np.where(amax > 0, byte, 1), 1, 254)
    scaled = (w * np.exp2(127.0 - byte)[:, None, :]).reshape(k, n).astype(np.float32)
    by_word = np.ascontiguousarray(scaled.reshape(k // 512, 128, 4, n).transpose(0, 1, 3, 2))
    if fmt == "e4m3":
        words = by_word.astype(ml_dtypes.float8_e4m3fn).view(np.uint8)
    else:
        c = by_word.astype(ml_dtypes.float4_e2m1fn).view(np.uint8) & 0xF
        words = c[..., 0::2] | (c[..., 1::2] << 4)
    return np.ascontiguousarray(words), np.ascontiguousarray(byte.astype(np.uint8).reshape(k // 512, 16, n))


def unpack_weight(words, scales, fmt):
    g, p, n, _ = words.shape
    if fmt == "e4m3":
        vals = np.ascontiguousarray(words).view(ml_dtypes.float8_e4m3fn).astype(np.float64)
    else:
        nib = np.empty((g, p, n, 4), np.uint8)
        nib[..., 0::2] = words & 0xF
        nib[..., 1::2] = words >> 4
        vals = E2M1[nib]
    vals = vals * np.repeat(np.exp2(scales.astype(np.float64) - 127.0), 8, axis=1)[..., None]
    return vals.transpose(0, 1, 3, 2).reshape(g * 512, n)


B, N, D, H = 8, 16, 128, 16384


def setup_inputs():
    t = mx_kscale(H)
    xi_p = bf(np.random.standard_normal((B, N, H)) * 0.7 * t)
    xj_p = bf(np.random.standard_normal((B, N, H)) * 0.7 * t)
    node_mask = bf(np.random.uniform(size=(B, N)) < 0.9)
    mb1 = bf(np.random.standard_normal(H) * 0.2 * t)
    mw2_words, mw2_scales = pack_weight(np.random.standard_normal((H, D)) * 0.5 / np.sqrt(H) / t[:, None], "e4m3")
    mb2 = bf(np.random.standard_normal(D) * 0.1)
    return {
        "xi_p": xi_p,
        "xj_p": xj_p,
        "node_mask": node_mask,
        "mb1": mb1,
        "mw2_words": mw2_words,
        "mw2_scales": mw2_scales,
        "mb2": mb2,
    }


def reference(xi_p, xj_p, node_mask, mb1, mw2_words, mw2_scales, mb2):
    mask = f64(node_mask)[..., None]
    h = np.maximum(f64(xi_p)[:, :, None, :] + f64(xj_p)[:, None, :, :] + f64(mb1), 0.0)
    msgs = np.maximum((mxq(h, 3, "e4m3") @ unpack_weight(mw2_words, mw2_scales, "e4m3")) + f64(mb2), 0.0)
    msgs = msgs * mask[:, None]
    return msgs.sum(axis=2)

@@ -1,0 +1,190 @@
+from contextlib import ExitStack
+
+import concourse.mybir as mybir
+from concourse.masks import make_identity
+
+F32 = mybir.dt.float32
+BF16 = mybir.dt.bfloat16
+I32 = mybir.dt.int32
+U8 = mybir.dt.uint8
+U32 = mybir.dt.uint32
+FP8X4 = mybir.dt.float8_e4m3fn_x4
+ADD = mybir.AluOpType.add
+MULT = mybir.AluOpType.mult
+RELU = mybir.ActivationFunctionType.Relu
+
+P = 128
+PACK = 4
+K_PASS = P * PACK
+GRAPHS = 8
+NODES = 16
+ROWS = GRAPHS * NODES
+HIDDEN = 16384
+D_OUT = 128
+PASSES = HIDDEN // K_PASS
+SHIFTS = NODES
+BANK_SHIFTS = 4
+BANKS = SHIFTS // BANK_SHIFTS
+BANK_COLS = BANK_SHIFTS * ROWS
+LOAD_PASSES = 4
+
+FLOPS = 2 * GRAPHS * NODES * NODES * HIDDEN * D_OUT
+
+
+def tile_graphdynamics_pa_k_kernel(
+    tc, xi_p, xj_p, node_mask, mb1, mw2_words, mw2_scales, mb2, out
+):
+    nc = tc.nc
+    xi_rows = xi_p.rearrange("b n h -> (b n) h")
+    xj_rows = xj_p.rearrange("b n h -> (b n) h")
+    out_rows = out.rearrange("b n d -> (b n) d")
+
+    with ExitStack() as stack:
+        const = stack.enter_context(tc.tile_pool(name="const", bufs=1))
+        loads = stack.enter_context(tc.tile_pool(name="loads", bufs=2))
+        operands = stack.enter_context(tc.tile_pool(name="operands", bufs=2))
+        hidden = stack.enter_context(tc.tile_pool(name="hidden", bufs=2))
+        quantised = stack.enter_context(tc.tile_pool(name="quantised", bufs=2))
+        acc_banks = stack.enter_context(tc.psum_pool(name="acc_banks", bufs=1))
+        work_banks = stack.enter_context(tc.psum_pool(name="work_banks", bufs=4))
+
+        mask_row = const.tile([P, GRAPHS, NODES], BF16)
+        nc.sync.dma_start(
+            out=mask_row[:].rearrange("p b n -> p (b n)"),
+            in_=node_mask.rearrange("b n -> (b n)").partition_broadcast(P),
+        )
+        mask_cols = const.tile([P, SHIFTS, GRAPHS, NODES], F32)
+        for s in range(SHIFTS):
+            nc.scalar.copy(out=mask_cols[:, s, :, 0 : NODES - s], in_=mask_row[:, :, s:NODES])
+            if s > 0:
+                nc.scalar.copy(out=mask_cols[:, s, :, NODES - s : NODES], in_=mask_row[:, :, 0:s])
+
+        mb2_bf16 = const.tile([D_OUT, 1], BF16)
+        nc.sync.dma_start(out=mb2_bf16[:], in_=mb2.rearrange("(d o) -> d o", o=1))
+        mb2_col = const.tile([D_OUT, 1], F32)
+        nc.vector.tensor_copy(out=mb2_col[:], in_=mb2_bf16[:])
+
+        ident = const.tile([P, P], F32)
+        make_identity(nc, ident[:])
+
+        w_words = const.tile([P, PASSES, PACK * D_OUT], U8, align_bytes=64)
+        w_scales = const.tile([P, PASSES, D_OUT], U8, align_bytes=64)
+        nc.vector.memset(w_scales[:].rearrange("p g n -> p (g n)").bitcast(I32), 0)
+
+        def load_weight():
+            for quadrant in range(4):
+                nc.sync.dma_start(
+                    out=w_scales[32 * quadrant : 32 * quadrant + 4, :, :].bitcast(I32),
+                    in_=mw2_scales[:, 4 * quadrant : 4 * quadrant + 4, :]
+                    .rearrange("g r n -> r g n")
+                    .bitcast(I32),
+                )
+            for g0 in range(0, PASSES, 8):
+                nc.sync.dma_start(
+                    out=w_words[:, g0 : g0 + 8, :].bitcast(I32),
+                    in_=mw2_words[g0 : g0 + 8].rearrange("g p n t -> p g (n t)").bitcast(I32),
+                )
+
+        acc = [acc_banks.tile([D_OUT, BANK_COLS], F32, name="acc%d" % q) for q in range(BANKS)]
+
+        for g in range(PASSES):
+            if g % LOAD_PASSES == 0:
+                k_cols = slice(g * K_PASS, (g + LOAD_PASSES) * K_PASS)
+                xi_nat = loads.tile([ROWS, LOAD_PASSES * K_PASS], BF16)
+                nc.sync.dma_start(out=xi_nat[:], in_=xi_rows[:, k_cols])
+                mb1_nat = loads.tile([ROWS, LOAD_PASSES * K_PASS], BF16)
+                nc.sync.dma_start(out=mb1_nat[:], in_=mb1[k_cols].partition_broadcast(ROWS))
+                xj_nat = loads.tile([ROWS, LOAD_PASSES * K_PASS], BF16)
+                nc.sync.dma_start(out=xj_nat[:], in_=xj_rows[:, k_cols])
+            if g == 0:
+                load_weight()
+            cols = slice((g % LOAD_PASSES) * K_PASS, (g % LOAD_PASSES + 1) * K_PASS)
+
+            xi_planes = operands.tile([ROWS, PACK, P], F32)
+            nc.vector.tensor_tensor(
+                out=xi_planes[:].rearrange("r t p -> r p t"),
+                in0=xi_nat[:, cols].rearrange("r (p t) -> r p t", t=PACK),
+                in1=mb1_nat[:, cols].rearrange("r (p t) -> r p t", t=PACK),
+                op=ADD,
+            )
+            xi_bank = work_banks.tile([P, PACK, ROWS], F32, tag="bank")
+            for t in range(PACK):
+                nc.tensor.transpose(xi_bank[:, t, :], xi_planes[:, t, :], ident[:])
+            xi_t = operands.tile([P, ROWS, PACK], F32)
+            nc.scalar.copy(out=xi_t[:], in_=xi_bank[:].rearrange("p t r -> p r t"))
+
+            xj_words = xj_nat[:, cols].bitcast(F32)
+            xj_bank = work_banks.tile([P, 2, ROWS], F32, tag="bank")
+            for u in range(2):
+                nc.tensor.transpose(xj_bank[:, u, :], xj_words[:, u : K_PASS // 2 : 2], ident[:])
+            xj_twice = operands.tile([P, GRAPHS, 2 * NODES, PACK], BF16)
+            xj_twice_words = (
+                xj_twice[:]
+                .rearrange("p b j t -> p (b j t)")
+                .bitcast(F32)
+                .rearrange("p (b j u) -> p b j u", b=GRAPHS, u=2)
+            )
+            for half in range(2):
+                nc.scalar.copy(
+                    out=xj_twice_words[:, :, half * NODES : (half + 1) * NODES, :],
+                    in_=xj_bank[:].rearrange("p u (b j) -> p b j u", b=GRAPHS),
+                )
+
+            h_sum = hidden.tile([P, SHIFTS, ROWS * PACK], BF16)
+            for s in range(SHIFTS):
+                nc.vector.tensor_tensor(
+                    out=h_sum[:, s, :].rearrange("p (b c) -> p b c", b=GRAPHS),
+                    in0=xi_t[:].rearrange("p (b i) t -> p b (i t)", b=GRAPHS),
+                    in1=xj_twice[:, :, s : s + NODES, :].rearrange("p b j t -> p b (j t)"),
+                    op=ADD,
+                )
+
+            h = hidden.tile([P, SHIFTS, ROWS * PACK], BF16, align_bytes=64)
+            h_codes = quantised.tile([P, BANKS, BANK_COLS], U32, align_bytes=64)
+            h_scales = quantised.tile([P, BANKS, BANK_COLS], U8, align_bytes=64)
+            for q in range(BANKS):
+                shifts = slice(q * BANK_SHIFTS, (q + 1) * BANK_SHIFTS)
+                nc.scalar.activation(out=h[:, shifts, :], in_=h_sum[:, shifts, :], func=RELU)
+                nc.vector.quantize_mx(
+                    out=h_codes[:, q, :].bitcast(FP8X4),
+                    scales=h_scales[:, q, :],
+                    in_=h[:, shifts, :].rearrange("p s c -> p (s c)"),
+                )
+                nc.tensor.matmul_mx(
+                    out=acc[q][:],
+                    lhsT=w_words[:, g, :].bitcast(FP8X4),
+                    lhsT_scale=w_scales[:, g, :],
+                    rhs=h_codes[:, q, :].bitcast(FP8X4),
+                    rhs_scale=h_scales[:, q, :],
+                    start=(g == 0),
+                    stop=(g == PASSES - 1),
+                )
+
+        msg = const.tile([D_OUT, SHIFTS, ROWS], F32)
+        for q in range(BANKS):
+            shifts = slice(q * BANK_SHIFTS, (q + 1) * BANK_SHIFTS)
+            nc.scalar.activation(
+                out=msg[:, shifts, :].rearrange("d s r -> d (s r)"),
+                in_=acc[q][:],
+                func=RELU,
+                bias=mb2_col[:, 0:1],
+            )
+            nc.vector.tensor_tensor(
+                out=msg[:, shifts, :],
+                in0=msg[:, shifts, :],
+                in1=mask_cols[:, shifts, :, :].rearrange("d s b i -> d s (b i)"),
+                op=MULT,
+            )
+        out_bank = work_banks.tile([ROWS, D_OUT], F32, tag="bank")
+        for s in range(SHIFTS):
+            nc.tensor.matmul(
+                out_bank[:],
+                lhsT=msg[:, s, :],
+                rhs=ident[:],
+                start=(s == 0),
+                stop=(s == SHIFTS - 1),
+                is_transpose=True,
+            )
+        out_sb = const.tile([ROWS, D_OUT], F32)
+        nc.vector.tensor_copy(out=out_sb[:], in_=out_bank[:])
+        nc.sync.dma_start(out=out_rows, in_=out_sb[:])

@@ -27,8 +27,18 @@ BANK_SHIFTS = 4
 BANKS = SHIFTS // BANK_SHIFTS
 BANK_COLS = BANK_SHIFTS * ROWS
 LOAD_PASSES = 4
+LOADS = PASSES // LOAD_PASSES
+
+TENSOR_SHIFTS = 9
+TENSOR_ONLY_BANKS = TENSOR_SHIFTS // BANK_SHIFTS
 
 FLOPS = 2 * GRAPHS * NODES * NODES * HIDDEN * D_OUT
+
+
+def rotate_senders(copy, dst, src, s):
+    copy(out=dst[:, :, 0 : NODES - s], in_=src[:, :, s:NODES])
+    if s > 0:
+        copy(out=dst[:, :, NODES - s : NODES], in_=src[:, :, 0:s])
 
 
 def tile_graphdynamics_pa_k_kernel(
@@ -41,83 +51,61 @@ def tile_graphdynamics_pa_k_kernel(
 
     with ExitStack() as stack:
         const = stack.enter_context(tc.tile_pool(name="const", bufs=1))
-        loads = stack.enter_context(tc.tile_pool(name="loads", bufs=2))
-        operands = stack.enter_context(tc.tile_pool(name="operands", bufs=2))
-        hidden = stack.enter_context(tc.tile_pool(name="hidden", bufs=2))
+        loads = stack.enter_context(tc.tile_pool(name="loads", bufs=3))
+        sorted_rows = stack.enter_context(tc.tile_pool(name="sorted_rows", bufs=3))
+        turned = stack.enter_context(tc.tile_pool(name="turned", bufs=2))
+        hidden = stack.enter_context(tc.tile_pool(name="hidden", bufs=3))
         quantised = stack.enter_context(tc.tile_pool(name="quantised", bufs=2))
         acc_banks = stack.enter_context(tc.psum_pool(name="acc_banks", bufs=1))
         work_banks = stack.enter_context(tc.psum_pool(name="work_banks", bufs=4))
+        stack.enter_context(tc.manual_schedule())
 
-        mask_row = const.tile([P, GRAPHS, NODES], BF16)
-        nc.sync.dma_start(
-            out=mask_row[:].rearrange("p b n -> p (b n)"),
-            in_=node_mask.rearrange("b n -> (b n)").partition_broadcast(P),
-        )
-        mask_cols = const.tile([P, SHIFTS, GRAPHS, NODES], F32)
-        for s in range(SHIFTS):
-            nc.scalar.copy(out=mask_cols[:, s, :, 0 : NODES - s], in_=mask_row[:, :, s:NODES])
-            if s > 0:
-                nc.scalar.copy(out=mask_cols[:, s, :, NODES - s : NODES], in_=mask_row[:, :, 0:s])
+        loaded = {}
+        planes = {}
+        operands = {}
+        h_tiles = {}
 
-        mb2_bf16 = const.tile([D_OUT, 1], BF16)
-        nc.sync.dma_start(out=mb2_bf16[:], in_=mb2.rearrange("(d o) -> d o", o=1))
-        mb2_col = const.tile([D_OUT, 1], F32)
-        nc.vector.tensor_copy(out=mb2_col[:], in_=mb2_bf16[:])
+        def load_rows(c):
+            k_cols = slice(c * LOAD_PASSES * K_PASS, (c + 1) * LOAD_PASSES * K_PASS)
+            xi_nat = loads.tile([ROWS, LOAD_PASSES * K_PASS], BF16)
+            nc.sync.dma_start(out=xi_nat[:], in_=xi_rows[:, k_cols])
+            mb1_nat = loads.tile([ROWS, LOAD_PASSES * K_PASS], BF16)
+            nc.sync.dma_start(out=mb1_nat[:], in_=mb1[k_cols].partition_broadcast(ROWS))
+            xj_nat = loads.tile([ROWS, LOAD_PASSES * K_PASS], BF16)
+            nc.sync.dma_start(out=xj_nat[:], in_=xj_rows[:, k_cols])
+            loaded[c] = (xi_nat, mb1_nat, xj_nat)
 
-        ident = const.tile([P, P], F32)
-        make_identity(nc, ident[:])
-
-        w_words = const.tile([P, PASSES, PACK * D_OUT], U8, align_bytes=64)
-        w_scales = const.tile([P, PASSES, D_OUT], U8, align_bytes=64)
-        nc.vector.memset(w_scales[:].rearrange("p g n -> p (g n)").bitcast(I32), 0)
-
-        def load_weight():
-            for quadrant in range(4):
-                nc.sync.dma_start(
-                    out=w_scales[32 * quadrant : 32 * quadrant + 4, :, :].bitcast(I32),
-                    in_=mw2_scales[:, 4 * quadrant : 4 * quadrant + 4, :]
-                    .rearrange("g r n -> r g n")
-                    .bitcast(I32),
-                )
-            for g0 in range(0, PASSES, 8):
-                nc.sync.dma_start(
-                    out=w_words[:, g0 : g0 + 8, :].bitcast(I32),
-                    in_=mw2_words[g0 : g0 + 8].rearrange("g p n t -> p g (n t)").bitcast(I32),
-                )
-
-        acc = [acc_banks.tile([D_OUT, BANK_COLS], F32, name="acc%d" % q) for q in range(BANKS)]
-
-        for g in range(PASSES):
-            if g % LOAD_PASSES == 0:
-                k_cols = slice(g * K_PASS, (g + LOAD_PASSES) * K_PASS)
-                xi_nat = loads.tile([ROWS, LOAD_PASSES * K_PASS], BF16)
-                nc.sync.dma_start(out=xi_nat[:], in_=xi_rows[:, k_cols])
-                mb1_nat = loads.tile([ROWS, LOAD_PASSES * K_PASS], BF16)
-                nc.sync.dma_start(out=mb1_nat[:], in_=mb1[k_cols].partition_broadcast(ROWS))
-                xj_nat = loads.tile([ROWS, LOAD_PASSES * K_PASS], BF16)
-                nc.sync.dma_start(out=xj_nat[:], in_=xj_rows[:, k_cols])
-            if g == 0:
-                load_weight()
+        def sort_rows(g):
+            if g % LOAD_PASSES == 0 and g // LOAD_PASSES + 1 < LOADS:
+                load_rows(g // LOAD_PASSES + 1)
+            xi_nat, mb1_nat, xj_nat = loaded[g // LOAD_PASSES]
             cols = slice((g % LOAD_PASSES) * K_PASS, (g % LOAD_PASSES + 1) * K_PASS)
-
-            xi_planes = operands.tile([ROWS, PACK, P], F32)
+            xi_planes = sorted_rows.tile([ROWS, PACK, P], F32)
             nc.vector.tensor_tensor(
                 out=xi_planes[:].rearrange("r t p -> r p t"),
                 in0=xi_nat[:, cols].rearrange("r (p t) -> r p t", t=PACK),
                 in1=mb1_nat[:, cols].rearrange("r (p t) -> r p t", t=PACK),
                 op=ADD,
             )
+            xj_planes = sorted_rows.tile([ROWS, PACK, P], F32)
+            nc.scalar.copy(
+                out=xj_planes[:].rearrange("r t p -> r p t"),
+                in_=xj_nat[:, cols].rearrange("r (p t) -> r p t", t=PACK),
+            )
+            planes[g] = (xi_planes, xj_planes, xj_nat[:, cols])
+
+        def turn_operands(g):
+            xi_planes, xj_planes, xj_bf16 = planes[g]
             xi_bank = work_banks.tile([P, PACK, ROWS], F32, tag="bank")
             for t in range(PACK):
                 nc.tensor.transpose(xi_bank[:, t, :], xi_planes[:, t, :], ident[:])
-            xi_t = operands.tile([P, ROWS, PACK], F32)
-            nc.scalar.copy(out=xi_t[:], in_=xi_bank[:].rearrange("p t r -> p r t"))
-
-            xj_words = xj_nat[:, cols].bitcast(F32)
+            xj_words = xj_bf16.bitcast(F32)
             xj_bank = work_banks.tile([P, 2, ROWS], F32, tag="bank")
             for u in range(2):
                 nc.tensor.transpose(xj_bank[:, u, :], xj_words[:, u : K_PASS // 2 : 2], ident[:])
-            xj_twice = operands.tile([P, GRAPHS, 2 * NODES, PACK], BF16)
+            xi_t = turned.tile([P, ROWS, PACK], F32)
+            nc.scalar.copy(out=xi_t[:], in_=xi_bank[:].rearrange("p t r -> p r t"))
+            xj_twice = turned.tile([P, GRAPHS, 2 * NODES, PACK], BF16)
             xj_twice_words = (
                 xj_twice[:]
                 .rearrange("p b j t -> p (b j t)")
@@ -129,37 +117,134 @@ def tile_graphdynamics_pa_k_kernel(
                     out=xj_twice_words[:, :, half * NODES : (half + 1) * NODES, :],
                     in_=xj_bank[:].rearrange("p u (b j) -> p b j u", b=GRAPHS),
                 )
+            operands[g] = (xi_t, xj_twice)
 
-            h_sum = hidden.tile([P, SHIFTS, ROWS * PACK], BF16)
-            for s in range(SHIFTS):
+        def tensor_line(g):
+            xi_planes, xj_planes, xj_bf16 = planes[g]
+            h = hidden.tile([P, SHIFTS, ROWS * PACK], BF16, align_bytes=64)
+            h_tiles[g] = h
+            for s in range(TENSOR_SHIFTS):
+                sum_bank = work_banks.tile([P, PACK, ROWS], F32, tag="bank")
+                for t in range(PACK):
+                    nc.tensor.matmul(
+                        sum_bank[:, t, :],
+                        lhsT=xi_planes[:, t, :],
+                        rhs=ident[:],
+                        start=True,
+                        stop=False,
+                        is_transpose=True,
+                    )
+                    nc.tensor.matmul(
+                        sum_bank[:, t, :],
+                        lhsT=xj_planes[:, t, :],
+                        rhs=shift_perm[:, s, :, :].rearrange("k b i -> k (b i)"),
+                        start=False,
+                        stop=True,
+                        is_transpose=True,
+                    )
+                nc.scalar.activation(
+                    out=h[:, s, :].rearrange("p (r t) -> p r t", t=PACK),
+                    in_=sum_bank[:].rearrange("p t r -> p r t"),
+                    func=RELU,
+                )
+
+        def vector_line_adds(g):
+            xi_t, xj_twice = operands[g]
+            h = h_tiles[g]
+            for s in range(TENSOR_SHIFTS, SHIFTS):
                 nc.vector.tensor_tensor(
-                    out=h_sum[:, s, :].rearrange("p (b c) -> p b c", b=GRAPHS),
+                    out=h[:, s, :].rearrange("p (b c) -> p b c", b=GRAPHS),
                     in0=xi_t[:].rearrange("p (b i) t -> p b (i t)", b=GRAPHS),
                     in1=xj_twice[:, :, s : s + NODES, :].rearrange("p b j t -> p b (j t)"),
                     op=ADD,
                 )
 
-            h = hidden.tile([P, SHIFTS, ROWS * PACK], BF16, align_bytes=64)
-            h_codes = quantised.tile([P, BANKS, BANK_COLS], U32, align_bytes=64)
-            h_scales = quantised.tile([P, BANKS, BANK_COLS], U8, align_bytes=64)
-            for q in range(BANKS):
-                shifts = slice(q * BANK_SHIFTS, (q + 1) * BANK_SHIFTS)
-                nc.scalar.activation(out=h[:, shifts, :], in_=h_sum[:, shifts, :], func=RELU)
-                nc.vector.quantize_mx(
-                    out=h_codes[:, q, :].bitcast(FP8X4),
-                    scales=h_scales[:, q, :],
-                    in_=h[:, shifts, :].rearrange("p s c -> p (s c)"),
-                )
-                nc.tensor.matmul_mx(
-                    out=acc[q][:],
-                    lhsT=w_words[:, g, :].bitcast(FP8X4),
-                    lhsT_scale=w_scales[:, g, :],
-                    rhs=h_codes[:, q, :].bitcast(FP8X4),
-                    rhs_scale=h_scales[:, q, :],
-                    start=(g == 0),
-                    stop=(g == PASSES - 1),
-                )
+        def vector_line_relu(g):
+            h_vector = h_tiles[g][:, TENSOR_SHIFTS:SHIFTS, :]
+            nc.vector.tensor_scalar_max(out=h_vector, in0=h_vector, scalar1=0.0)
 
+        def quantise_and_multiply(g, q):
+            if q == 0:
+                h_codes = quantised.tile([P, BANKS, BANK_COLS], U32, align_bytes=64)
+                h_scales = quantised.tile([P, BANKS, BANK_COLS], U8, align_bytes=64)
+                mx_tiles[g] = (h_codes, h_scales)
+            h_codes, h_scales = mx_tiles[g]
+            shifts = slice(q * BANK_SHIFTS, (q + 1) * BANK_SHIFTS)
+            nc.vector.quantize_mx(
+                out=h_codes[:, q, :].bitcast(FP8X4),
+                scales=h_scales[:, q, :],
+                in_=h_tiles[g][:, shifts, :].rearrange("p s c -> p (s c)"),
+            )
+            nc.tensor.matmul_mx(
+                out=acc[q][:],
+                lhsT=w_words[:, g, :].bitcast(FP8X4),
+                lhsT_scale=w_scales[:, g, :],
+                rhs=h_codes[:, q, :].bitcast(FP8X4),
+                rhs_scale=h_scales[:, q, :],
+                start=(g == 0),
+                stop=(g == PASSES - 1),
+            )
+
+        mx_tiles = {}
+
+        load_rows(0)
+
+        w_words = const.tile([P, PASSES, PACK * D_OUT], U8, align_bytes=64)
+        w_scales = const.tile([P, PASSES, D_OUT], U8, align_bytes=64)
+        nc.vector.memset(w_scales[:].rearrange("p g n -> p (g n)").bitcast(I32), 0)
+        for quadrant in range(4):
+            nc.sync.dma_start(
+                out=w_scales[32 * quadrant : 32 * quadrant + 4, :, :].bitcast(I32),
+                in_=mw2_scales[:, 4 * quadrant : 4 * quadrant + 4, :]
+                .rearrange("g r n -> r g n")
+                .bitcast(I32),
+            )
+        for g0 in range(0, PASSES, 8):
+            nc.sync.dma_start(
+                out=w_words[:, g0 : g0 + 8, :].bitcast(I32),
+                in_=mw2_words[g0 : g0 + 8].rearrange("g p n t -> p g (n t)").bitcast(I32),
+            )
+        mask_row = const.tile([P, GRAPHS, NODES], BF16)
+        nc.sync.dma_start(
+            out=mask_row[:].rearrange("p b n -> p (b n)"),
+            in_=node_mask.rearrange("b n -> (b n)").partition_broadcast(P),
+        )
+        mb2_bf16 = const.tile([D_OUT, 1], BF16)
+        nc.sync.dma_start(out=mb2_bf16[:], in_=mb2.rearrange("(d o) -> d o", o=1))
+
+        ident = const.tile([P, P], F32)
+        make_identity(nc, ident[:])
+        shift_perm = const.tile([ROWS, TENSOR_SHIFTS, GRAPHS, NODES], F32)
+        for s in range(TENSOR_SHIFTS):
+            rotate_senders(
+                nc.vector.tensor_copy,
+                shift_perm[:, s, :, :],
+                ident[:].rearrange("k (b i) -> k b i", b=GRAPHS),
+                s,
+            )
+        mask_cols = const.tile([P, SHIFTS, GRAPHS, NODES], F32)
+        for s in range(SHIFTS):
+            rotate_senders(nc.gpsimd.tensor_copy, mask_cols[:, s, :, :], mask_row[:], s)
+
+        acc = [acc_banks.tile([D_OUT, BANK_COLS], F32, name="acc%d" % q) for q in range(BANKS)]
+
+        for r in range(-2, PASSES):
+            if 0 <= r + 1 < PASSES:
+                turn_operands(r + 1)
+                tensor_line(r + 1)
+            if r >= 0:
+                vector_line_adds(r)
+                for q in range(TENSOR_ONLY_BANKS):
+                    quantise_and_multiply(r, q)
+                vector_line_relu(r)
+            if r + 2 < PASSES:
+                sort_rows(r + 2)
+            if r >= 0:
+                for q in range(TENSOR_ONLY_BANKS, BANKS):
+                    quantise_and_multiply(r, q)
+
+        mb2_col = const.tile([D_OUT, 1], F32)
+        nc.vector.tensor_copy(out=mb2_col[:], in_=mb2_bf16[:])
         msg = const.tile([D_OUT, SHIFTS, ROWS], F32)
         for q in range(BANKS):
             shifts = slice(q * BANK_SHIFTS, (q + 1) * BANK_SHIFTS)

@@ -26,8 +26,11 @@ SHIFTS = NODES
 BANK_SHIFTS = 4
 BANKS = SHIFTS // BANK_SHIFTS
 BANK_COLS = BANK_SHIFTS * ROWS
+QUADRANT = 32
+QUADRANT_SCALES = 4
 LOAD_PASSES = 4
 LOADS = PASSES // LOAD_PASSES
+WEIGHT_LOAD_PASSES = 8
 
 TENSOR_SHIFTS = 9
 TENSOR_ONLY_BANKS = TENSOR_SHIFTS // BANK_SHIFTS
@@ -64,44 +67,53 @@ def tile_graphdynamics_pa_k_kernel(
         planes = {}
         operands = {}
         h_tiles = {}
+        mx_tiles = {}
 
-        def load_rows(c):
-            k_cols = slice(c * LOAD_PASSES * K_PASS, (c + 1) * LOAD_PASSES * K_PASS)
+        def load_rows(c, cuts):
             xi_nat = loads.tile([ROWS, LOAD_PASSES * K_PASS], BF16)
-            nc.sync.dma_start(out=xi_nat[:], in_=xi_rows[:, k_cols])
             mb1_nat = loads.tile([ROWS, LOAD_PASSES * K_PASS], BF16)
-            nc.sync.dma_start(out=mb1_nat[:], in_=mb1[k_cols].partition_broadcast(ROWS))
             xj_nat = loads.tile([ROWS, LOAD_PASSES * K_PASS], BF16)
-            nc.sync.dma_start(out=xj_nat[:], in_=xj_rows[:, k_cols])
             loaded[c] = (xi_nat, mb1_nat, xj_nat)
+            width = LOAD_PASSES * K_PASS // cuts
+            for cut in range(cuts):
+                cols = slice(cut * width, (cut + 1) * width)
+                k_first = c * LOAD_PASSES * K_PASS + cut * width
+                k_cols = slice(k_first, k_first + width)
+                nc.sync.dma_start(out=xi_nat[:, cols], in_=xi_rows[:, k_cols])
+                nc.sync.dma_start(out=mb1_nat[:, cols], in_=mb1[k_cols].partition_broadcast(ROWS))
+                nc.sync.dma_start(out=xj_nat[:, cols], in_=xj_rows[:, k_cols])
+
+        def rows_of_pass(g):
+            cols = slice((g % LOAD_PASSES) * K_PASS, (g % LOAD_PASSES + 1) * K_PASS)
+            xi_nat, mb1_nat, xj_nat = loaded[g // LOAD_PASSES]
+            return xi_nat[:, cols], mb1_nat[:, cols], xj_nat[:, cols]
 
         def sort_rows(g):
             if g % LOAD_PASSES == 0 and g // LOAD_PASSES + 1 < LOADS:
-                load_rows(g // LOAD_PASSES + 1)
-            xi_nat, mb1_nat, xj_nat = loaded[g // LOAD_PASSES]
-            cols = slice((g % LOAD_PASSES) * K_PASS, (g % LOAD_PASSES + 1) * K_PASS)
+                load_rows(g // LOAD_PASSES + 1, cuts=1)
+            xi_bf16, mb1_bf16, xj_bf16 = rows_of_pass(g)
             xi_planes = sorted_rows.tile([ROWS, PACK, P], F32)
             nc.vector.tensor_tensor(
                 out=xi_planes[:].rearrange("r t p -> r p t"),
-                in0=xi_nat[:, cols].rearrange("r (p t) -> r p t", t=PACK),
-                in1=mb1_nat[:, cols].rearrange("r (p t) -> r p t", t=PACK),
+                in0=xi_bf16.rearrange("r (p t) -> r p t", t=PACK),
+                in1=mb1_bf16.rearrange("r (p t) -> r p t", t=PACK),
                 op=ADD,
             )
             xj_planes = sorted_rows.tile([ROWS, PACK, P], F32)
             nc.scalar.copy(
                 out=xj_planes[:].rearrange("r t p -> r p t"),
-                in_=xj_nat[:, cols].rearrange("r (p t) -> r p t", t=PACK),
+                in_=xj_bf16.rearrange("r (p t) -> r p t", t=PACK),
             )
-            planes[g] = (xi_planes, xj_planes, xj_nat[:, cols])
+            planes[g] = (xi_planes, xj_planes)
 
         def turn_operands(g):
-            xi_planes, xj_planes, xj_bf16 = planes[g]
+            xi_planes = planes[g][0]
             xi_bank = work_banks.tile([P, PACK, ROWS], F32, tag="bank")
             for t in range(PACK):
                 nc.tensor.transpose(xi_bank[:, t, :], xi_planes[:, t, :], ident[:])
-            xj_words = xj_bf16.bitcast(F32)
-            xj_bank = work_banks.tile([P, 2, ROWS], F32, tag="bank")
-            for u in range(2):
+            xj_words = rows_of_pass(g)[2].bitcast(F32)
+            xj_bank = work_banks.tile([P, PACK // 2, ROWS], F32, tag="bank")
+            for u in range(PACK // 2):
                 nc.tensor.transpose(xj_bank[:, u, :], xj_words[:, u : K_PASS // 2 : 2], ident[:])
             xi_t = turned.tile([P, ROWS, PACK], F32)
             nc.scalar.copy(out=xi_t[:], in_=xi_bank[:].rearrange("p t r -> p r t"))
@@ -110,7 +122,7 @@ def tile_graphdynamics_pa_k_kernel(
                 xj_twice[:]
                 .rearrange("p b j t -> p (b j t)")
                 .bitcast(F32)
-                .rearrange("p (b j u) -> p b j u", b=GRAPHS, u=2)
+                .rearrange("p (b j u) -> p b j u", b=GRAPHS, u=PACK // 2)
             )
             for half in range(2):
                 nc.scalar.copy(
@@ -120,7 +132,7 @@ def tile_graphdynamics_pa_k_kernel(
             operands[g] = (xi_t, xj_twice)
 
         def tensor_line(g):
-            xi_planes, xj_planes, xj_bf16 = planes[g]
+            xi_planes, xj_planes = planes[g]
             h = hidden.tile([P, SHIFTS, ROWS * PACK], BF16, align_bytes=64)
             h_tiles[g] = h
             for s in range(TENSOR_SHIFTS):
@@ -150,10 +162,9 @@ def tile_graphdynamics_pa_k_kernel(
 
         def vector_line_adds(g):
             xi_t, xj_twice = operands[g]
-            h = h_tiles[g]
             for s in range(TENSOR_SHIFTS, SHIFTS):
                 nc.vector.tensor_tensor(
-                    out=h[:, s, :].rearrange("p (b c) -> p b c", b=GRAPHS),
+                    out=h_tiles[g][:, s, :].rearrange("p (b c) -> p b c", b=GRAPHS),
                     in0=xi_t[:].rearrange("p (b i) t -> p b (i t)", b=GRAPHS),
                     in1=xj_twice[:, :, s : s + NODES, :].rearrange("p b j t -> p b (j t)"),
                     op=ADD,
@@ -185,32 +196,33 @@ def tile_graphdynamics_pa_k_kernel(
                 stop=(g == PASSES - 1),
             )
 
-        mx_tiles = {}
-
-        load_rows(0)
-
-        w_words = const.tile([P, PASSES, PACK * D_OUT], U8, align_bytes=64)
-        w_scales = const.tile([P, PASSES, D_OUT], U8, align_bytes=64)
-        nc.vector.memset(w_scales[:].rearrange("p g n -> p (g n)").bitcast(I32), 0)
-        for quadrant in range(4):
-            nc.sync.dma_start(
-                out=w_scales[32 * quadrant : 32 * quadrant + 4, :, :].bitcast(I32),
-                in_=mw2_scales[:, 4 * quadrant : 4 * quadrant + 4, :]
-                .rearrange("g r n -> r g n")
-                .bitcast(I32),
-            )
-        for g0 in range(0, PASSES, 8):
-            nc.sync.dma_start(
-                out=w_words[:, g0 : g0 + 8, :].bitcast(I32),
-                in_=mw2_words[g0 : g0 + 8].rearrange("g p n t -> p g (n t)").bitcast(I32),
-            )
+        mb2_bf16 = const.tile([D_OUT, 1], BF16)
+        nc.sync.dma_start(out=mb2_bf16[:], in_=mb2.rearrange("(d o) -> d o", o=1))
         mask_row = const.tile([P, GRAPHS, NODES], BF16)
         nc.sync.dma_start(
             out=mask_row[:].rearrange("p b n -> p (b n)"),
             in_=node_mask.rearrange("b n -> (b n)").partition_broadcast(P),
         )
-        mb2_bf16 = const.tile([D_OUT, 1], BF16)
-        nc.sync.dma_start(out=mb2_bf16[:], in_=mb2.rearrange("(d o) -> d o", o=1))
+        load_rows(0, cuts=LOAD_PASSES)
+        w_words = const.tile([P, PASSES, PACK * D_OUT], U8, align_bytes=64)
+        w_scales = const.tile([P, PASSES, D_OUT], U8, align_bytes=64)
+        nc.vector.memset(w_scales[:].rearrange("p g n -> p (g n)").bitcast(I32), 0)
+        for quadrant in range(P // QUADRANT):
+            first_row = quadrant * QUADRANT_SCALES
+            first_partition = quadrant * QUADRANT
+            nc.sync.dma_start(
+                out=w_scales[first_partition : first_partition + QUADRANT_SCALES, :, :].bitcast(I32),
+                in_=mw2_scales[:, first_row : first_row + QUADRANT_SCALES, :]
+                .rearrange("g r n -> r g n")
+                .bitcast(I32),
+            )
+        for g0 in range(0, PASSES, WEIGHT_LOAD_PASSES):
+            nc.sync.dma_start(
+                out=w_words[:, g0 : g0 + WEIGHT_LOAD_PASSES, :].bitcast(I32),
+                in_=mw2_words[g0 : g0 + WEIGHT_LOAD_PASSES]
+                .rearrange("g p n t -> p g (n t)")
+                .bitcast(I32),
+            )
 
         ident = const.tile([P, P], F32)
         make_identity(nc, ident[:])
@@ -222,6 +234,8 @@ def tile_graphdynamics_pa_k_kernel(
                 ident[:].rearrange("k (b i) -> k b i", b=GRAPHS),
                 s,
             )
+        mb2_col = const.tile([D_OUT, 1], F32)
+        nc.vector.tensor_copy(out=mb2_col[:], in_=mb2_bf16[:])
         mask_cols = const.tile([P, SHIFTS, GRAPHS, NODES], F32)
         for s in range(SHIFTS):
             rotate_senders(nc.gpsimd.tensor_copy, mask_cols[:, s, :, :], mask_row[:], s)
@@ -243,8 +257,6 @@ def tile_graphdynamics_pa_k_kernel(
                 for q in range(TENSOR_ONLY_BANKS, BANKS):
                     quantise_and_multiply(r, q)
 
-        mb2_col = const.tile([D_OUT, 1], F32)
-        nc.vector.tensor_copy(out=mb2_col[:], in_=mb2_bf16[:])
         msg = const.tile([D_OUT, SHIFTS, ROWS], F32)
         for q in range(BANKS):
             shifts = slice(q * BANK_SHIFTS, (q + 1) * BANK_SHIFTS)

@@ -32,10 +32,16 @@ LOAD_PASSES = 4
 LOADS = PASSES // LOAD_PASSES
 WEIGHT_LOAD_PASSES = 8
 
-TENSOR_SHIFTS = 9
-TENSOR_ONLY_BANKS = TENSOR_SHIFTS // BANK_SHIFTS
+MAX_TENSOR_SHIFTS = 9
+VECTOR_RELU_FIRST = 10
+SCALAR_RELU_PLACE = 2
+TENSOR_ONLY_BANKS = 2
 
 FLOPS = 2 * GRAPHS * NODES * NODES * HIDDEN * D_OUT
+
+
+def tensor_shifts(g):
+    return MAX_TENSOR_SHIFTS - g % 2
 
 
 def rotate_senders(copy, dst, src, s):
@@ -58,7 +64,7 @@ def tile_graphdynamics_pa_k_kernel(
         sorted_rows = stack.enter_context(tc.tile_pool(name="sorted_rows", bufs=3))
         turned = stack.enter_context(tc.tile_pool(name="turned", bufs=2))
         hidden = stack.enter_context(tc.tile_pool(name="hidden", bufs=3))
-        quantised = stack.enter_context(tc.tile_pool(name="quantised", bufs=2))
+        quantised = stack.enter_context(tc.tile_pool(name="quantised", bufs=3))
         acc_banks = stack.enter_context(tc.psum_pool(name="acc_banks", bufs=1))
         work_banks = stack.enter_context(tc.psum_pool(name="work_banks", bufs=4))
         stack.enter_context(tc.manual_schedule())
@@ -92,19 +98,23 @@ def tile_graphdynamics_pa_k_kernel(
             if g % LOAD_PASSES == 0 and g // LOAD_PASSES + 1 < LOADS:
                 load_rows(g // LOAD_PASSES + 1, cuts=1)
             xi_bf16, mb1_bf16, xj_bf16 = rows_of_pass(g)
+            xj_planes = sorted_rows.tile([ROWS, PACK, P], F32)
+            nc.scalar.copy(
+                out=xj_planes[:].rearrange("r t p -> r p t"),
+                in_=xj_bf16.rearrange("r (p t) -> r p t", t=PACK),
+            )
             xi_planes = sorted_rows.tile([ROWS, PACK, P], F32)
+            planes[g] = (xi_planes, xj_planes)
+            return xi_planes, xi_bf16, mb1_bf16
+
+        def sort_sums(sums):
+            xi_planes, xi_bf16, mb1_bf16 = sums
             nc.vector.tensor_tensor(
                 out=xi_planes[:].rearrange("r t p -> r p t"),
                 in0=xi_bf16.rearrange("r (p t) -> r p t", t=PACK),
                 in1=mb1_bf16.rearrange("r (p t) -> r p t", t=PACK),
                 op=ADD,
             )
-            xj_planes = sorted_rows.tile([ROWS, PACK, P], F32)
-            nc.scalar.copy(
-                out=xj_planes[:].rearrange("r t p -> r p t"),
-                in_=xj_bf16.rearrange("r (p t) -> r p t", t=PACK),
-            )
-            planes[g] = (xi_planes, xj_planes)
 
         def turn_operands(g):
             xi_planes = planes[g][0]
@@ -131,11 +141,12 @@ def tile_graphdynamics_pa_k_kernel(
                 )
             operands[g] = (xi_t, xj_twice)
 
-        def tensor_line(g):
+        def tensor_line(g, first, end):
             xi_planes, xj_planes = planes[g]
-            h = hidden.tile([P, SHIFTS, ROWS * PACK], BF16, align_bytes=64)
-            h_tiles[g] = h
-            for s in range(TENSOR_SHIFTS):
+            if first == 0:
+                h_tiles[g] = hidden.tile([P, SHIFTS, ROWS * PACK], BF16, align_bytes=64, name="h")
+            h = h_tiles[g]
+            for s in range(first, end):
                 sum_bank = work_banks.tile([P, PACK, ROWS], F32, tag="bank")
                 for t in range(PACK):
                     nc.tensor.matmul(
@@ -162,7 +173,7 @@ def tile_graphdynamics_pa_k_kernel(
 
         def vector_line_adds(g):
             xi_t, xj_twice = operands[g]
-            for s in range(TENSOR_SHIFTS, SHIFTS):
+            for s in range(tensor_shifts(g), SHIFTS):
                 nc.vector.tensor_tensor(
                     out=h_tiles[g][:, s, :].rearrange("p (b c) -> p b c", b=GRAPHS),
                     in0=xi_t[:].rearrange("p (b i) t -> p b (i t)", b=GRAPHS),
@@ -170,11 +181,16 @@ def tile_graphdynamics_pa_k_kernel(
                     op=ADD,
                 )
 
-        def vector_line_relu(g):
-            h_vector = h_tiles[g][:, TENSOR_SHIFTS:SHIFTS, :]
+        def scalar_relu(g):
+            for s in range(tensor_shifts(g), VECTOR_RELU_FIRST):
+                h_shift = h_tiles[g][:, s, :]
+                nc.scalar.activation(out=h_shift, in_=h_shift, func=RELU)
+
+        def vector_relu(g):
+            h_vector = h_tiles[g][:, VECTOR_RELU_FIRST:SHIFTS, :]
             nc.vector.tensor_scalar_max(out=h_vector, in0=h_vector, scalar1=0.0)
 
-        def quantise_and_multiply(g, q):
+        def quantise(g, q):
             if q == 0:
                 h_codes = quantised.tile([P, BANKS, BANK_COLS], U32, align_bytes=64)
                 h_scales = quantised.tile([P, BANKS, BANK_COLS], U8, align_bytes=64)
@@ -186,15 +202,19 @@ def tile_graphdynamics_pa_k_kernel(
                 scales=h_scales[:, q, :],
                 in_=h_tiles[g][:, shifts, :].rearrange("p s c -> p (s c)"),
             )
-            nc.tensor.matmul_mx(
-                out=acc[q][:],
-                lhsT=w_words[:, g, :].bitcast(FP8X4),
-                lhsT_scale=w_scales[:, g, :],
-                rhs=h_codes[:, q, :].bitcast(FP8X4),
-                rhs_scale=h_scales[:, q, :],
-                start=(g == 0),
-                stop=(g == PASSES - 1),
-            )
+
+        def multiply(g):
+            h_codes, h_scales = mx_tiles[g]
+            for q in range(BANKS):
+                nc.tensor.matmul_mx(
+                    out=acc[q][:],
+                    lhsT=w_words[:, g, :].bitcast(FP8X4),
+                    lhsT_scale=w_scales[:, g, :],
+                    rhs=h_codes[:, q, :].bitcast(FP8X4),
+                    rhs_scale=h_scales[:, q, :],
+                    start=(g == 0),
+                    stop=(g == PASSES - 1),
+                )
 
         mb2_bf16 = const.tile([D_OUT, 1], BF16)
         nc.sync.dma_start(out=mb2_bf16[:], in_=mb2.rearrange("(d o) -> d o", o=1))
@@ -226,8 +246,8 @@ def tile_graphdynamics_pa_k_kernel(
 
         ident = const.tile([P, P], F32)
         make_identity(nc, ident[:])
-        shift_perm = const.tile([ROWS, TENSOR_SHIFTS, GRAPHS, NODES], F32)
-        for s in range(TENSOR_SHIFTS):
+        shift_perm = const.tile([ROWS, MAX_TENSOR_SHIFTS, GRAPHS, NODES], F32)
+        for s in range(MAX_TENSOR_SHIFTS):
             rotate_senders(
                 nc.vector.tensor_copy,
                 shift_perm[:, s, :, :],
@@ -242,20 +262,32 @@ def tile_graphdynamics_pa_k_kernel(
 
         acc = [acc_banks.tile([D_OUT, BANK_COLS], F32, name="acc%d" % q) for q in range(BANKS)]
 
-        for r in range(-2, PASSES):
-            if 0 <= r + 1 < PASSES:
-                turn_operands(r + 1)
-                tensor_line(r + 1)
-            if r >= 0:
+        for r in range(-2, PASSES + 1):
+            vector_runs = 0 <= r < PASSES
+            tensor_runs = 0 <= r + 1 < PASSES
+            sums = None
+            if vector_runs:
                 vector_line_adds(r)
-                for q in range(TENSOR_ONLY_BANKS):
-                    quantise_and_multiply(r, q)
-                vector_line_relu(r)
+            if r >= 1:
+                multiply(r - 1)
             if r + 2 < PASSES:
-                sort_rows(r + 2)
-            if r >= 0:
+                sums = sort_rows(r + 2)
+            if tensor_runs:
+                turn_operands(r + 1)
+                tensor_line(r + 1, 0, SCALAR_RELU_PLACE)
+            if vector_runs:
+                scalar_relu(r)
+            if tensor_runs:
+                tensor_line(r + 1, SCALAR_RELU_PLACE, tensor_shifts(r + 1))
+            if vector_runs:
+                for q in range(TENSOR_ONLY_BANKS):
+                    quantise(r, q)
+                vector_relu(r)
+            if sums:
+                sort_sums(sums)
+            if vector_runs:
                 for q in range(TENSOR_ONLY_BANKS, BANKS):
-                    quantise_and_multiply(r, q)
+                    quantise(r, q)
 
         msg = const.tile([D_OUT, SHIFTS, ROWS], F32)
         for q in range(BANKS):

@@ -32,16 +32,18 @@ LOAD_PASSES = 4
 LOADS = PASSES // LOAD_PASSES
 WEIGHT_LOAD_PASSES = 8
 
-MAX_TENSOR_SHIFTS = 9
-VECTOR_RELU_FIRST = 10
+TENSOR_SHIFTS = 8
+LAST_EXTRA_SHIFTS = 3
+VECTOR_SHIFTS = SHIFTS - TENSOR_SHIFTS
+SHIFT_COLS = (GRAPHS - 1) * NODES * PACK
+PLAIN_FIRST = VECTOR_SHIFTS * SHIFT_COLS
+SCALAR_RELU_SHIFTS = 1
+PLAIN_RING = 3
+PLAIN_MB1_ROW = 2 * NODES
 SCALAR_RELU_PLACE = 2
 TENSOR_ONLY_BANKS = 2
 
 FLOPS = 2 * GRAPHS * NODES * NODES * HIDDEN * D_OUT
-
-
-def tensor_shifts(g):
-    return MAX_TENSOR_SHIFTS - g % 2
 
 
 def rotate_senders(copy, dst, src, s):
@@ -89,6 +91,17 @@ def tile_graphdynamics_pa_k_kernel(
                 nc.sync.dma_start(out=mb1_nat[:, cols], in_=mb1[k_cols].partition_broadcast(ROWS))
                 nc.sync.dma_start(out=xj_nat[:, cols], in_=xj_rows[:, k_cols])
 
+        def load_plain_rows(c):
+            k_first = c * LOAD_PASSES * K_PASS
+            k_cols = slice(k_first, k_first + LOAD_PASSES * K_PASS)
+            rows = plain_rows[c % PLAIN_RING]
+            nc.sync.dma_start(out=rows[0:NODES, :], in_=xi_rows[0:NODES, k_cols])
+            nc.sync.dma_start(out=rows[NODES : 2 * NODES, :], in_=xj_rows[0:NODES, k_cols])
+            nc.sync.dma_start(
+                out=rows[PLAIN_MB1_ROW : PLAIN_MB1_ROW + 1, :],
+                in_=mb1[k_cols].rearrange("(o k) -> o k", o=1),
+            )
+
         def rows_of_pass(g):
             cols = slice((g % LOAD_PASSES) * K_PASS, (g % LOAD_PASSES + 1) * K_PASS)
             xi_nat, mb1_nat, xj_nat = loaded[g // LOAD_PASSES]
@@ -97,6 +110,7 @@ def tile_graphdynamics_pa_k_kernel(
         def sort_rows(g):
             if g % LOAD_PASSES == 0 and g // LOAD_PASSES + 1 < LOADS:
                 load_rows(g // LOAD_PASSES + 1, cuts=1)
+                load_plain_rows(g // LOAD_PASSES + 1)
             xi_bf16, mb1_bf16, xj_bf16 = rows_of_pass(g)
             xj_planes = sorted_rows.tile([ROWS, PACK, P], F32)
             nc.scalar.copy(
@@ -126,7 +140,10 @@ def tile_graphdynamics_pa_k_kernel(
             for u in range(PACK // 2):
                 nc.tensor.transpose(xj_bank[:, u, :], xj_words[:, u : K_PASS // 2 : 2], ident[:])
             xi_t = turned.tile([P, ROWS, PACK], F32)
-            nc.scalar.copy(out=xi_t[:], in_=xi_bank[:].rearrange("p t r -> p r t"))
+            nc.scalar.copy(
+                out=xi_t[:, NODES:ROWS, :],
+                in_=xi_bank[:, :, NODES:ROWS].rearrange("p t r -> p r t"),
+            )
             xj_twice = turned.tile([P, GRAPHS, 2 * NODES, PACK], BF16)
             xj_twice_words = (
                 xj_twice[:]
@@ -136,15 +153,53 @@ def tile_graphdynamics_pa_k_kernel(
             )
             for half in range(2):
                 nc.scalar.copy(
-                    out=xj_twice_words[:, :, half * NODES : (half + 1) * NODES, :],
-                    in_=xj_bank[:].rearrange("p u (b j) -> p b j u", b=GRAPHS),
+                    out=xj_twice_words[:, 1:GRAPHS, half * NODES : (half + 1) * NODES, :],
+                    in_=xj_bank[:, :, NODES:ROWS].rearrange("p u (b j) -> p b j u", b=GRAPHS - 1),
                 )
             operands[g] = (xi_t, xj_twice)
 
+        def plain_line(g):
+            rows = plain_rows[g // LOAD_PASSES % PLAIN_RING]
+            k_first = g % LOAD_PASSES * K_PASS
+            plain_bank = work_banks.tile([P, PACK, ROWS], F32, tag="bank")
+            for t in range(PACK):
+                nc.tensor.matmul(
+                    plain_bank[:, t, :],
+                    lhsT=rows[:, k_first + t : k_first + K_PASS : PACK],
+                    rhs=plain_select[:].rearrange("k s i -> k (s i)"),
+                    start=True,
+                    stop=True,
+                )
+            nc.scalar.activation(
+                out=vector_h(g)[:, PLAIN_FIRST:].rearrange("p (r t) -> p r t", t=PACK),
+                in_=plain_bank[:].rearrange("p t r -> p r t"),
+                func=RELU,
+            )
+
+        def build_plain_select():
+            for v in range(VECTOR_SHIFTS):
+                s = TENSOR_SHIFTS + v
+                for first, end, sender in ((0, NODES - s, s), (NODES - s, NODES, 0)):
+                    nc.vector.scalar_tensor_tensor(
+                        out=plain_select[:, v, first:end],
+                        in0=ident[:, first:end],
+                        scalar=ident[:, PLAIN_MB1_ROW : PLAIN_MB1_ROW + 1],
+                        in1=ident[:, NODES + sender : NODES + sender + end - first],
+                        op0=ADD,
+                        op1=ADD,
+                    )
+
+        def vector_h(g):
+            return h_tiles[g][:, TENSOR_SHIFTS:SHIFTS, :].rearrange("p s c -> p (s c)")
+
+        def vector_shift(g, v):
+            return vector_h(g)[:, v * SHIFT_COLS : (v + 1) * SHIFT_COLS]
+
+        def first_vector_shift(g):
+            return LAST_EXTRA_SHIFTS if g == PASSES - 1 else 0
+
         def tensor_line(g, first, end):
             xi_planes, xj_planes = planes[g]
-            if first == 0:
-                h_tiles[g] = hidden.tile([P, SHIFTS, ROWS * PACK], BF16, align_bytes=64, name="h")
             h = h_tiles[g]
             for s in range(first, end):
                 sum_bank = work_banks.tile([P, PACK, ROWS], F32, tag="bank")
@@ -165,29 +220,39 @@ def tile_graphdynamics_pa_k_kernel(
                         stop=True,
                         is_transpose=True,
                     )
+                if s < TENSOR_SHIFTS:
+                    h_shift, first_row = h[:, s, :], 0
+                else:
+                    h_shift, first_row = vector_shift(g, s - TENSOR_SHIFTS), NODES
                 nc.scalar.activation(
-                    out=h[:, s, :].rearrange("p (r t) -> p r t", t=PACK),
-                    in_=sum_bank[:].rearrange("p t r -> p r t"),
+                    out=h_shift.rearrange("p (r t) -> p r t", t=PACK),
+                    in_=sum_bank[:, :, first_row:ROWS].rearrange("p t r -> p r t"),
                     func=RELU,
                 )
 
         def vector_line_adds(g):
             xi_t, xj_twice = operands[g]
-            for s in range(tensor_shifts(g), SHIFTS):
+            for v in range(first_vector_shift(g), VECTOR_SHIFTS):
+                s = TENSOR_SHIFTS + v
                 nc.vector.tensor_tensor(
-                    out=h_tiles[g][:, s, :].rearrange("p (b c) -> p b c", b=GRAPHS),
-                    in0=xi_t[:].rearrange("p (b i) t -> p b (i t)", b=GRAPHS),
-                    in1=xj_twice[:, :, s : s + NODES, :].rearrange("p b j t -> p b (j t)"),
+                    out=vector_shift(g, v).rearrange(
+                        "p (b c) -> p b c", b=GRAPHS - 1
+                    ),
+                    in0=xi_t[:, NODES:ROWS, :].rearrange("p (b i) t -> p b (i t)", b=GRAPHS - 1),
+                    in1=xj_twice[:, 1:GRAPHS, s : s + NODES, :].rearrange("p b j t -> p b (j t)"),
                     op=ADD,
                 )
 
         def scalar_relu(g):
-            for s in range(tensor_shifts(g), VECTOR_RELU_FIRST):
-                h_shift = h_tiles[g][:, s, :]
-                nc.scalar.activation(out=h_shift, in_=h_shift, func=RELU)
+            first = first_vector_shift(g)
+            h_scalar = vector_h(g)[
+                :, first * SHIFT_COLS : (first + SCALAR_RELU_SHIFTS) * SHIFT_COLS
+            ]
+            nc.scalar.activation(out=h_scalar, in_=h_scalar, func=RELU)
 
         def vector_relu(g):
-            h_vector = h_tiles[g][:, VECTOR_RELU_FIRST:SHIFTS, :]
+            first = first_vector_shift(g) + SCALAR_RELU_SHIFTS
+            h_vector = vector_h(g)[:, first * SHIFT_COLS : PLAIN_FIRST]
             nc.vector.tensor_scalar_max(out=h_vector, in0=h_vector, scalar1=0.0)
 
         def quantise(g, q):
@@ -216,6 +281,9 @@ def tile_graphdynamics_pa_k_kernel(
                     stop=(g == PASSES - 1),
                 )
 
+        ident = const.tile([P, P], F32)
+        make_identity(nc, ident[:])
+
         mb2_bf16 = const.tile([D_OUT, 1], BF16)
         nc.sync.dma_start(out=mb2_bf16[:], in_=mb2.rearrange("(d o) -> d o", o=1))
         mask_row = const.tile([P, GRAPHS, NODES], BF16)
@@ -223,10 +291,16 @@ def tile_graphdynamics_pa_k_kernel(
             out=mask_row[:].rearrange("p b n -> p (b n)"),
             in_=node_mask.rearrange("b n -> (b n)").partition_broadcast(P),
         )
+        plain_rows = []
+        for i in range(PLAIN_RING):
+            rows = const.tile([P, LOAD_PASSES * K_PASS], BF16, name="plain_rows%d" % i)
+            nc.vector.memset(rows[:].bitcast(I32), 0)
+            plain_rows.append(rows)
         load_rows(0, cuts=LOAD_PASSES)
+        load_plain_rows(0)
         w_words = const.tile([P, PASSES, PACK * D_OUT], U8, align_bytes=64)
         w_scales = const.tile([P, PASSES, D_OUT], U8, align_bytes=64)
-        nc.vector.memset(w_scales[:].rearrange("p g n -> p (g n)").bitcast(I32), 0)
+        nc.gpsimd.memset(w_scales[:].rearrange("p g n -> p (g n)").bitcast(I32), 0)
         for quadrant in range(P // QUADRANT):
             first_row = quadrant * QUADRANT_SCALES
             first_partition = quadrant * QUADRANT
@@ -244,16 +318,15 @@ def tile_graphdynamics_pa_k_kernel(
                 .bitcast(I32),
             )
 
-        ident = const.tile([P, P], F32)
-        make_identity(nc, ident[:])
-        shift_perm = const.tile([ROWS, MAX_TENSOR_SHIFTS, GRAPHS, NODES], F32)
-        for s in range(MAX_TENSOR_SHIFTS):
+        shift_perm = const.tile([ROWS, TENSOR_SHIFTS + LAST_EXTRA_SHIFTS, GRAPHS, NODES], F32)
+        for s in range(TENSOR_SHIFTS + LAST_EXTRA_SHIFTS):
             rotate_senders(
                 nc.vector.tensor_copy,
                 shift_perm[:, s, :, :],
                 ident[:].rearrange("k (b i) -> k b i", b=GRAPHS),
                 s,
             )
+        plain_select = const.tile([P, VECTOR_SHIFTS, NODES], BF16)
         mb2_col = const.tile([D_OUT, 1], F32)
         nc.vector.tensor_copy(out=mb2_col[:], in_=mb2_bf16[:])
         mask_cols = const.tile([P, SHIFTS, GRAPHS, NODES], F32)
@@ -272,13 +345,22 @@ def tile_graphdynamics_pa_k_kernel(
                 multiply(r - 1)
             if r + 2 < PASSES:
                 sums = sort_rows(r + 2)
+            if r == -1:
+                build_plain_select()
             if tensor_runs:
+                h_tiles[r + 1] = hidden.tile(
+                    [P, SHIFTS, ROWS * PACK], BF16, align_bytes=64, name="h"
+                )
+                if r >= 0:
+                    plain_line(r + 1)
                 turn_operands(r + 1)
                 tensor_line(r + 1, 0, SCALAR_RELU_PLACE)
+                if r < 0:
+                    plain_line(r + 1)
             if vector_runs:
                 scalar_relu(r)
             if tensor_runs:
-                tensor_line(r + 1, SCALAR_RELU_PLACE, tensor_shifts(r + 1))
+                tensor_line(r + 1, SCALAR_RELU_PLACE, TENSOR_SHIFTS + first_vector_shift(r + 1))
             if vector_runs:
                 for q in range(TENSOR_ONLY_BANKS):
                     quantise(r, q)
@@ -289,26 +371,44 @@ def tile_graphdynamics_pa_k_kernel(
                 for q in range(TENSOR_ONLY_BANKS, BANKS):
                     quantise(r, q)
 
-        msg = const.tile([D_OUT, SHIFTS, ROWS], F32)
+        product = const.tile([D_OUT, SHIFTS, ROWS], F32)
+        msg = const.tile([D_OUT, SHIFTS, GRAPHS, NODES], F32)
         for q in range(BANKS):
             shifts = slice(q * BANK_SHIFTS, (q + 1) * BANK_SHIFTS)
             nc.scalar.activation(
-                out=msg[:, shifts, :].rearrange("d s r -> d (s r)"),
+                out=product[:, shifts, :].rearrange("d s r -> d (s r)"),
                 in_=acc[q][:],
                 func=RELU,
                 bias=mb2_col[:, 0:1],
             )
-            nc.vector.tensor_tensor(
-                out=msg[:, shifts, :],
-                in0=msg[:, shifts, :],
-                in1=mask_cols[:, shifts, :, :].rearrange("d s b i -> d s (b i)"),
-                op=MULT,
-            )
+            if q < TENSOR_ONLY_BANKS:
+                nc.vector.tensor_tensor(
+                    out=msg[:, shifts, :, :].rearrange("d s b i -> d s (b i)"),
+                    in0=product[:, shifts, :],
+                    in1=mask_cols[:, shifts, :, :].rearrange("d s b i -> d s (b i)"),
+                    op=MULT,
+                )
+        product_vector = product[:, TENSOR_SHIFTS:SHIFTS, :].rearrange("d s r -> d (s r)")
+        plain_col = PLAIN_FIRST // PACK
+        nc.vector.tensor_tensor(
+            out=msg[:, TENSOR_SHIFTS:SHIFTS, 1:GRAPHS, :],
+            in0=product_vector[:, 0:plain_col].rearrange(
+                "d (s b i) -> d s b i", s=VECTOR_SHIFTS, b=GRAPHS - 1
+            ),
+            in1=mask_cols[:, TENSOR_SHIFTS:SHIFTS, 1:GRAPHS, :],
+            op=MULT,
+        )
+        nc.vector.tensor_tensor(
+            out=msg[:, TENSOR_SHIFTS:SHIFTS, 0, :],
+            in0=product_vector[:, plain_col:].rearrange("d (s i) -> d s i", s=VECTOR_SHIFTS),
+            in1=mask_cols[:, TENSOR_SHIFTS:SHIFTS, 0, :],
+            op=MULT,
+        )
         out_bank = work_banks.tile([ROWS, D_OUT], F32, tag="bank")
         for s in range(SHIFTS):
             nc.tensor.matmul(
                 out_bank[:],
-                lhsT=msg[:, s, :],
+                lhsT=msg[:, s, :, :].rearrange("d b i -> d (b i)"),
                 rhs=ident[:],
                 start=(s == 0),
                 stop=(s == SHIFTS - 1),

@@ -18,38 +18,50 @@ PACK = 4
 K_PASS = P * PACK
 GRAPHS = 8
 NODES = 16
+HALVES = 2
+HALF = NODES // HALVES
 ROWS = GRAPHS * NODES
 HIDDEN = 16384
 D_OUT = 128
 PASSES = HIDDEN // K_PASS
-SHIFTS = NODES
-BANK_SHIFTS = 4
-BANKS = SHIFTS // BANK_SHIFTS
-BANK_COLS = BANK_SHIFTS * ROWS
+PART_COLS = HALF * ROWS
+BANK_COLS = 512
+PART_BANKS = PART_COLS // BANK_COLS
 QUADRANT = 32
 QUADRANT_SCALES = 4
 LOAD_PASSES = 4
 LOADS = PASSES // LOAD_PASSES
+LOAD_COLS = LOAD_PASSES * K_PASS
 WEIGHT_LOAD_PASSES = 8
 
-TENSOR_SHIFTS = 8
-LAST_EXTRA_SHIFTS = 3
-VECTOR_SHIFTS = SHIFTS - TENSOR_SHIFTS
-SHIFT_COLS = (GRAPHS - 1) * NODES * PACK
-PLAIN_FIRST = VECTOR_SHIFTS * SHIFT_COLS
-SCALAR_RELU_SHIFTS = 1
+VECTOR_GRAPHS = GRAPHS - 1
+HALF_COLS = HALF * VECTOR_GRAPHS * HALF
+VECTOR_COLS = HALVES * HALF_COLS
+PLAIN_GRAPHS = 1
+LAST_PLAIN_GRAPHS = 3
+PLAIN_XJ_ROW = LAST_PLAIN_GRAPHS * NODES
+PLAIN_MB1_ROW = 2 * LAST_PLAIN_GRAPHS * NODES
 PLAIN_RING = 3
-PLAIN_MB1_ROW = 2 * NODES
+SCALAR_RELU_SENDERS = 4
+SCALAR_RELU_COLS = SCALAR_RELU_SENDERS * VECTOR_GRAPHS * HALF
 SCALAR_RELU_PLACE = 2
-TENSOR_ONLY_BANKS = 2
 
 FLOPS = 2 * GRAPHS * NODES * NODES * HIDDEN * D_OUT
 
 
-def rotate_senders(copy, dst, src, s):
-    copy(out=dst[:, :, 0 : NODES - s], in_=src[:, :, s:NODES])
-    if s > 0:
-        copy(out=dst[:, :, NODES - s : NODES], in_=src[:, :, 0:s])
+def plain_graphs(g):
+    return LAST_PLAIN_GRAPHS if g == PASSES - 1 else PLAIN_GRAPHS
+
+
+def rotate_in_halves(copy, dst, src, d):
+    copy(out=dst[:, :, 0 : HALF - d], in_=src[:, :, d:HALF])
+    if d > 0:
+        copy(out=dst[:, :, HALF - d : HALF], in_=src[:, :, 0:d])
+
+
+def swap_halves(copy, dst, src):
+    for half in range(HALVES):
+        copy(out=dst[:, :, half, :], in_=src[:, :, 1 - half, :])
 
 
 def tile_graphdynamics_pa_k_kernel(
@@ -78,25 +90,26 @@ def tile_graphdynamics_pa_k_kernel(
         mx_tiles = {}
 
         def load_rows(c, cuts):
-            xi_nat = loads.tile([ROWS, LOAD_PASSES * K_PASS], BF16)
-            mb1_nat = loads.tile([ROWS, LOAD_PASSES * K_PASS], BF16)
-            xj_nat = loads.tile([ROWS, LOAD_PASSES * K_PASS], BF16)
+            xi_nat = loads.tile([ROWS, LOAD_COLS], BF16)
+            mb1_nat = loads.tile([ROWS, LOAD_COLS], BF16)
+            xj_nat = loads.tile([ROWS, LOAD_COLS], BF16)
             loaded[c] = (xi_nat, mb1_nat, xj_nat)
-            width = LOAD_PASSES * K_PASS // cuts
+            width = LOAD_COLS // cuts
             for cut in range(cuts):
                 cols = slice(cut * width, (cut + 1) * width)
-                k_first = c * LOAD_PASSES * K_PASS + cut * width
+                k_first = c * LOAD_COLS + cut * width
                 k_cols = slice(k_first, k_first + width)
                 nc.sync.dma_start(out=xi_nat[:, cols], in_=xi_rows[:, k_cols])
                 nc.sync.dma_start(out=mb1_nat[:, cols], in_=mb1[k_cols].partition_broadcast(ROWS))
                 nc.sync.dma_start(out=xj_nat[:, cols], in_=xj_rows[:, k_cols])
 
         def load_plain_rows(c):
-            k_first = c * LOAD_PASSES * K_PASS
-            k_cols = slice(k_first, k_first + LOAD_PASSES * K_PASS)
+            k_cols = slice(c * LOAD_COLS, (c + 1) * LOAD_COLS)
             rows = plain_rows[c % PLAIN_RING]
-            nc.sync.dma_start(out=rows[0:NODES, :], in_=xi_rows[0:NODES, k_cols])
-            nc.sync.dma_start(out=rows[NODES : 2 * NODES, :], in_=xj_rows[0:NODES, k_cols])
+            nc.sync.dma_start(out=rows[0:PLAIN_XJ_ROW, :], in_=xi_rows[0:PLAIN_XJ_ROW, k_cols])
+            nc.sync.dma_start(
+                out=rows[PLAIN_XJ_ROW:PLAIN_MB1_ROW, :], in_=xj_rows[0:PLAIN_XJ_ROW, k_cols]
+            )
             nc.sync.dma_start(
                 out=rows[PLAIN_MB1_ROW : PLAIN_MB1_ROW + 1, :],
                 in_=mb1[k_cols].rearrange("(o k) -> o k", o=1),
@@ -107,101 +120,87 @@ def tile_graphdynamics_pa_k_kernel(
             xi_nat, mb1_nat, xj_nat = loaded[g // LOAD_PASSES]
             return xi_nat[:, cols], mb1_nat[:, cols], xj_nat[:, cols]
 
-        def sort_rows(g):
+        def sort_senders(g):
             if g % LOAD_PASSES == 0 and g // LOAD_PASSES + 1 < LOADS:
                 load_rows(g // LOAD_PASSES + 1, cuts=1)
                 load_plain_rows(g // LOAD_PASSES + 1)
-            xi_bf16, mb1_bf16, xj_bf16 = rows_of_pass(g)
+            xi_planes = sorted_rows.tile([ROWS, PACK, P], F32)
             xj_planes = sorted_rows.tile([ROWS, PACK, P], F32)
+            planes[g] = (xi_planes, xj_planes)
             nc.scalar.copy(
                 out=xj_planes[:].rearrange("r t p -> r p t"),
-                in_=xj_bf16.rearrange("r (p t) -> r p t", t=PACK),
+                in_=rows_of_pass(g)[2].rearrange("r (p t) -> r p t", t=PACK),
             )
-            xi_planes = sorted_rows.tile([ROWS, PACK, P], F32)
-            planes[g] = (xi_planes, xj_planes)
-            return xi_planes, xi_bf16, mb1_bf16
 
-        def sort_sums(sums):
-            xi_planes, xi_bf16, mb1_bf16 = sums
+        def sort_receivers(g):
+            xi_bf16, mb1_bf16, xj_bf16 = rows_of_pass(g)
             nc.vector.tensor_tensor(
-                out=xi_planes[:].rearrange("r t p -> r p t"),
+                out=planes[g][0][:].rearrange("r t p -> r p t"),
                 in0=xi_bf16.rearrange("r (p t) -> r p t", t=PACK),
                 in1=mb1_bf16.rearrange("r (p t) -> r p t", t=PACK),
                 op=ADD,
             )
 
         def turn_operands(g):
+            first = plain_graphs(g)
+            graphs = GRAPHS - first
             xi_planes = planes[g][0]
             xi_bank = work_banks.tile([P, PACK, ROWS], F32, tag="bank")
             for t in range(PACK):
-                nc.tensor.transpose(xi_bank[:, t, :], xi_planes[:, t, :], ident[:])
+                nc.tensor.transpose(xi_bank[:, t, :], xi_planes[:, t, :], by_half[:])
             xj_words = rows_of_pass(g)[2].bitcast(F32)
             xj_bank = work_banks.tile([P, PACK // 2, ROWS], F32, tag="bank")
             for u in range(PACK // 2):
                 nc.tensor.transpose(xj_bank[:, u, :], xj_words[:, u : K_PASS // 2 : 2], ident[:])
-            xi_t = turned.tile([P, ROWS, PACK], F32)
+            xi_t = turned.tile([P, HALVES * VECTOR_GRAPHS * HALF * PACK], F32)
+            xi_view = xi_t[:, 0 : HALVES * graphs * HALF * PACK]
             nc.scalar.copy(
-                out=xi_t[:, NODES:ROWS, :],
-                in_=xi_bank[:, :, NODES:ROWS].rearrange("p t r -> p r t"),
+                out=xi_view.rearrange("p (h c t) -> p h c t", h=HALVES, t=PACK),
+                in_=xi_bank[:].rearrange("p t (h c) -> p h c t", h=HALVES)[:, :, first * HALF :, :],
             )
-            xj_twice = turned.tile([P, GRAPHS, 2 * NODES, PACK], BF16)
-            xj_twice_words = (
-                xj_twice[:]
-                .rearrange("p b j t -> p (b j t)")
-                .bitcast(F32)
-                .rearrange("p (b j u) -> p b j u", b=GRAPHS, u=PACK // 2)
+            xj_t = turned.tile([P, NODES * VECTOR_GRAPHS * PACK], BF16)
+            xj_view = xj_t[:, 0 : NODES * graphs * PACK]
+            nc.scalar.copy(
+                out=xj_view.bitcast(F32).rearrange("p (j b u) -> p j b u", j=NODES, b=graphs),
+                in_=xj_bank[:].rearrange("p u (b j) -> p j b u", b=GRAPHS)[:, :, first:, :],
             )
-            for half in range(2):
-                nc.scalar.copy(
-                    out=xj_twice_words[:, 1:GRAPHS, half * NODES : (half + 1) * NODES, :],
-                    in_=xj_bank[:, :, NODES:ROWS].rearrange("p u (b j) -> p b j u", b=GRAPHS - 1),
-                )
-            operands[g] = (xi_t, xj_twice)
+            operands[g] = (
+                xi_view.rearrange("p (h b i t) -> p h b i t", h=HALVES, b=graphs, t=PACK),
+                xj_view.rearrange("p (j b t) -> p j b t", j=NODES, b=graphs),
+            )
 
         def plain_line(g):
             rows = plain_rows[g // LOAD_PASSES % PLAIN_RING]
             k_first = g % LOAD_PASSES * K_PASS
-            plain_bank = work_banks.tile([P, PACK, ROWS], F32, tag="bank")
-            for t in range(PACK):
-                nc.tensor.matmul(
-                    plain_bank[:, t, :],
-                    lhsT=rows[:, k_first + t : k_first + K_PASS : PACK],
-                    rhs=plain_select[:].rearrange("k s i -> k (s i)"),
-                    start=True,
-                    stop=True,
-                )
-            nc.scalar.activation(
-                out=vector_h(g)[:, PLAIN_FIRST:].rearrange("p (r t) -> p r t", t=PACK),
-                in_=plain_bank[:].rearrange("p t r -> p r t"),
-                func=RELU,
-            )
-
-        def build_plain_select():
-            for v in range(VECTOR_SHIFTS):
-                s = TENSOR_SHIFTS + v
-                for first, end, sender in ((0, NODES - s, s), (NODES - s, NODES, 0)):
-                    nc.vector.scalar_tensor_tensor(
-                        out=plain_select[:, v, first:end],
-                        in0=ident[:, first:end],
-                        scalar=ident[:, PLAIN_MB1_ROW : PLAIN_MB1_ROW + 1],
-                        in1=ident[:, NODES + sender : NODES + sender + end - first],
-                        op0=ADD,
-                        op1=ADD,
+            h_same = h_tiles[g][1]
+            for b in range(plain_graphs(g)):
+                bank = work_banks.tile([P, PACK, ROWS], F32, tag="bank")
+                for t in range(PACK):
+                    nc.tensor.matmul(
+                        bank[:, t, :],
+                        lhsT=rows[:, k_first + t : k_first + K_PASS : PACK],
+                        rhs=plain_select[:, b, :, :, :].rearrange("k h j i -> k (h j i)"),
+                        start=True,
+                        stop=True,
                     )
-
-        def vector_h(g):
-            return h_tiles[g][:, TENSOR_SHIFTS:SHIFTS, :].rearrange("p s c -> p (s c)")
-
-        def vector_shift(g, v):
-            return vector_h(g)[:, v * SHIFT_COLS : (v + 1) * SHIFT_COLS]
-
-        def first_vector_shift(g):
-            return LAST_EXTRA_SHIFTS if g == PASSES - 1 else 0
+                if b == 0:
+                    h_graph = h_same[:, VECTOR_COLS * PACK :].rearrange(
+                        "p (n c) -> p n c", n=NODES
+                    )
+                else:
+                    h_graph = h_same[:, 0 : VECTOR_COLS * PACK].rearrange(
+                        "p (n b c) -> p n b c", n=NODES, b=VECTOR_GRAPHS
+                    )[:, :, b - 1, :]
+                nc.scalar.activation(
+                    out=h_graph.rearrange("p n (i t) -> p n i t", t=PACK),
+                    in_=bank[:].rearrange("p t (n i) -> p n i t", n=NODES),
+                    func=RELU,
+                )
 
         def tensor_line(g, first, end):
             xi_planes, xj_planes = planes[g]
-            h = h_tiles[g]
-            for s in range(first, end):
+            h_cross = h_tiles[g][0]
+            for d in range(first, end):
                 sum_bank = work_banks.tile([P, PACK, ROWS], F32, tag="bank")
                 for t in range(PACK):
                     nc.tensor.matmul(
@@ -215,86 +214,77 @@ def tile_graphdynamics_pa_k_kernel(
                     nc.tensor.matmul(
                         sum_bank[:, t, :],
                         lhsT=xj_planes[:, t, :],
-                        rhs=shift_perm[:, s, :, :].rearrange("k b i -> k (b i)"),
+                        rhs=cross_perm[:, d, :, :].rearrange("k n i -> k (n i)"),
                         start=False,
                         stop=True,
                         is_transpose=True,
                     )
-                if s < TENSOR_SHIFTS:
-                    h_shift, first_row = h[:, s, :], 0
-                else:
-                    h_shift, first_row = vector_shift(g, s - TENSOR_SHIFTS), NODES
                 nc.scalar.activation(
-                    out=h_shift.rearrange("p (r t) -> p r t", t=PACK),
-                    in_=sum_bank[:, :, first_row:ROWS].rearrange("p t r -> p r t"),
+                    out=h_cross[:, d * ROWS * PACK : (d + 1) * ROWS * PACK].rearrange(
+                        "p (r t) -> p r t", t=PACK
+                    ),
+                    in_=sum_bank[:].rearrange("p t r -> p r t"),
                     func=RELU,
                 )
 
         def vector_line_adds(g):
-            xi_t, xj_twice = operands[g]
-            for v in range(first_vector_shift(g), VECTOR_SHIFTS):
-                s = TENSOR_SHIFTS + v
+            xi_t, xj_t = operands[g]
+            first = plain_graphs(g)
+            shape = [P, HALF, GRAPHS - first, HALF, PACK]
+            for half in range(HALVES):
+                h_half = h_tiles[g][1][:, half * HALF_COLS * PACK : (half + 1) * HALF_COLS * PACK]
                 nc.vector.tensor_tensor(
-                    out=vector_shift(g, v).rearrange(
-                        "p (b c) -> p b c", b=GRAPHS - 1
-                    ),
-                    in0=xi_t[:, NODES:ROWS, :].rearrange("p (b i) t -> p b (i t)", b=GRAPHS - 1),
-                    in1=xj_twice[:, 1:GRAPHS, s : s + NODES, :].rearrange("p b j t -> p b (j t)"),
+                    out=h_half.rearrange("p (j b i t) -> p j b i t", j=HALF, b=VECTOR_GRAPHS, t=PACK)[
+                        :, :, first - 1 :, :, :
+                    ],
+                    in0=xi_t[:, half, :, :, :].unsqueeze(1).to_broadcast(shape),
+                    in1=xj_t[:, half * HALF : (half + 1) * HALF, :, :].unsqueeze(3).to_broadcast(shape),
                     op=ADD,
                 )
 
         def scalar_relu(g):
-            first = first_vector_shift(g)
-            h_scalar = vector_h(g)[
-                :, first * SHIFT_COLS : (first + SCALAR_RELU_SHIFTS) * SHIFT_COLS
-            ]
+            h_scalar = h_tiles[g][1][:, 0 : SCALAR_RELU_COLS * PACK]
             nc.scalar.activation(out=h_scalar, in_=h_scalar, func=RELU)
 
         def vector_relu(g):
-            first = first_vector_shift(g) + SCALAR_RELU_SHIFTS
-            h_vector = vector_h(g)[:, first * SHIFT_COLS : PLAIN_FIRST]
+            h_vector = h_tiles[g][1][:, SCALAR_RELU_COLS * PACK : VECTOR_COLS * PACK]
             nc.vector.tensor_scalar_max(out=h_vector, in0=h_vector, scalar1=0.0)
 
-        def quantise(g, q):
-            if q == 0:
-                h_codes = quantised.tile([P, BANKS, BANK_COLS], U32, align_bytes=64)
-                h_scales = quantised.tile([P, BANKS, BANK_COLS], U8, align_bytes=64)
-                mx_tiles[g] = (h_codes, h_scales)
-            h_codes, h_scales = mx_tiles[g]
-            shifts = slice(q * BANK_SHIFTS, (q + 1) * BANK_SHIFTS)
+        def quantise(g, part):
+            h_codes = quantised.tile([P, PART_COLS], U32, align_bytes=64, tag="codes%d" % part)
+            h_scales = quantised.tile([P, PART_COLS], U8, align_bytes=64, tag="scales%d" % part)
+            mx_tiles[g, part] = (h_codes, h_scales)
             nc.vector.quantize_mx(
-                out=h_codes[:, q, :].bitcast(FP8X4),
-                scales=h_scales[:, q, :],
-                in_=h_tiles[g][:, shifts, :].rearrange("p s c -> p (s c)"),
+                out=h_codes[:].bitcast(FP8X4), scales=h_scales[:], in_=h_tiles[g][part][:]
             )
 
         def multiply(g):
-            h_codes, h_scales = mx_tiles[g]
-            for q in range(BANKS):
+            for q in range(2 * PART_BANKS):
+                h_codes, h_scales = mx_tiles[g, q // PART_BANKS]
+                cols = slice(q % PART_BANKS * BANK_COLS, (q % PART_BANKS + 1) * BANK_COLS)
                 nc.tensor.matmul_mx(
                     out=acc[q][:],
                     lhsT=w_words[:, g, :].bitcast(FP8X4),
                     lhsT_scale=w_scales[:, g, :],
-                    rhs=h_codes[:, q, :].bitcast(FP8X4),
-                    rhs_scale=h_scales[:, q, :],
+                    rhs=h_codes[:, cols].bitcast(FP8X4),
+                    rhs_scale=h_scales[:, cols],
                     start=(g == 0),
                     stop=(g == PASSES - 1),
                 )
 
         ident = const.tile([P, P], F32)
         make_identity(nc, ident[:])
-
         mb2_bf16 = const.tile([D_OUT, 1], BF16)
         nc.sync.dma_start(out=mb2_bf16[:], in_=mb2.rearrange("(d o) -> d o", o=1))
-        mask_row = const.tile([P, GRAPHS, NODES], BF16)
+        mask_row = const.tile([P, GRAPHS, HALVES, HALF], BF16)
         nc.sync.dma_start(
-            out=mask_row[:].rearrange("p b n -> p (b n)"),
+            out=mask_row[:].rearrange("p b h i -> p (b h i)"),
             in_=node_mask.rearrange("b n -> (b n)").partition_broadcast(P),
         )
         plain_rows = []
         for i in range(PLAIN_RING):
-            rows = const.tile([P, LOAD_PASSES * K_PASS], BF16, name="plain_rows%d" % i)
-            nc.vector.memset(rows[:].bitcast(I32), 0)
+            rows = const.tile([P, LOAD_COLS], BF16, name="plain_rows%d" % i)
+            (nc.vector if i == 0 else nc.gpsimd).memset(rows[:].bitcast(I32), 0)
             plain_rows.append(rows)
         load_rows(0, cuts=LOAD_PASSES)
         load_plain_rows(0)
@@ -318,39 +308,75 @@ def tile_graphdynamics_pa_k_kernel(
                 .bitcast(I32),
             )
 
-        shift_perm = const.tile([ROWS, TENSOR_SHIFTS + LAST_EXTRA_SHIFTS, GRAPHS, NODES], F32)
-        for s in range(TENSOR_SHIFTS + LAST_EXTRA_SHIFTS):
-            rotate_senders(
-                nc.vector.tensor_copy,
-                shift_perm[:, s, :, :],
-                ident[:].rearrange("k (b i) -> k b i", b=GRAPHS),
-                s,
-            )
-        plain_select = const.tile([P, VECTOR_SHIFTS, NODES], BF16)
+        by_half = const.tile([P, P], F32)
+        nc.vector.tensor_copy(
+            out=by_half[:].rearrange("k (h b i) -> k h b i", h=HALVES, b=GRAPHS),
+            in_=ident[:].rearrange("k (b h i) -> k h b i", h=HALVES, b=GRAPHS),
+        )
+        cross_perm = const.tile([ROWS, HALF, GRAPHS * HALVES, HALF], F32)
+        swap_halves(
+            nc.vector.tensor_copy,
+            cross_perm[:, 0, :, :].rearrange("k (b h) i -> k b h i", h=HALVES),
+            ident[:].rearrange("k (b h i) -> k b h i", h=HALVES, b=GRAPHS),
+        )
+        for d in range(1, HALF):
+            rotate_in_halves(nc.vector.tensor_copy, cross_perm[:, d, :, :], cross_perm[:, 0, :, :], d)
+        plain_select = const.tile([P, LAST_PLAIN_GRAPHS, HALVES, HALF, HALF], BF16)
+
+        def build_plain_select():
+            for b in range(LAST_PLAIN_GRAPHS):
+                for half in range(HALVES):
+                    xi_first = b * NODES + half * HALF
+                    xj_first = PLAIN_XJ_ROW + xi_first
+                    nc.vector.scalar_tensor_tensor(
+                        out=plain_select[:, b, half, :, :],
+                        in0=ident[:, xi_first : xi_first + HALF]
+                        .unsqueeze(1)
+                        .to_broadcast([P, HALF, HALF]),
+                        scalar=ident[:, PLAIN_MB1_ROW : PLAIN_MB1_ROW + 1],
+                        in1=ident[:, xj_first : xj_first + HALF]
+                        .unsqueeze(2)
+                        .to_broadcast([P, HALF, HALF]),
+                        op0=ADD,
+                        op1=ADD,
+                    )
+
         mb2_col = const.tile([D_OUT, 1], F32)
         nc.vector.tensor_copy(out=mb2_col[:], in_=mb2_bf16[:])
-        mask_cols = const.tile([P, SHIFTS, GRAPHS, NODES], F32)
-        for s in range(SHIFTS):
-            rotate_senders(nc.gpsimd.tensor_copy, mask_cols[:, s, :, :], mask_row[:], s)
+        mask_cross = const.tile([P, HALF, GRAPHS * HALVES, HALF], F32)
+        swap_halves(
+            nc.gpsimd.tensor_copy,
+            mask_cross[:, 0, :, :].rearrange("p (b h) i -> p b h i", h=HALVES),
+            mask_row[:],
+        )
+        for d in range(1, HALF):
+            rotate_in_halves(nc.gpsimd.tensor_copy, mask_cross[:, d, :, :], mask_cross[:, 0, :, :], d)
+        mask_same = const.tile([P, HALVES, HALF, GRAPHS], F32)
+        nc.gpsimd.tensor_copy(
+            out=mask_same[:].rearrange("p h j b -> p (h j) b"),
+            in_=mask_row[:].rearrange("p b h j -> p (h j) b"),
+        )
 
-        acc = [acc_banks.tile([D_OUT, BANK_COLS], F32, name="acc%d" % q) for q in range(BANKS)]
+        acc = [
+            acc_banks.tile([D_OUT, BANK_COLS], F32, name="acc%d" % q) for q in range(2 * PART_BANKS)
+        ]
 
         for r in range(-2, PASSES + 1):
             vector_runs = 0 <= r < PASSES
             tensor_runs = 0 <= r + 1 < PASSES
-            sums = None
+            sort_runs = r + 2 < PASSES
             if vector_runs:
                 vector_line_adds(r)
             if r >= 1:
                 multiply(r - 1)
-            if r + 2 < PASSES:
-                sums = sort_rows(r + 2)
+            if sort_runs:
+                sort_senders(r + 2)
             if r == -1:
                 build_plain_select()
             if tensor_runs:
-                h_tiles[r + 1] = hidden.tile(
-                    [P, SHIFTS, ROWS * PACK], BF16, align_bytes=64, name="h"
-                )
+                h_cross = hidden.tile([P, PART_COLS * PACK], BF16, align_bytes=64)
+                h_same = hidden.tile([P, PART_COLS * PACK], BF16, align_bytes=64)
+                h_tiles[r + 1] = (h_cross, h_same)
                 if r >= 0:
                     plain_line(r + 1)
                 turn_operands(r + 1)
@@ -360,58 +386,55 @@ def tile_graphdynamics_pa_k_kernel(
             if vector_runs:
                 scalar_relu(r)
             if tensor_runs:
-                tensor_line(r + 1, SCALAR_RELU_PLACE, TENSOR_SHIFTS + first_vector_shift(r + 1))
+                tensor_line(r + 1, SCALAR_RELU_PLACE, HALF)
+            if sort_runs:
+                sort_receivers(r + 2)
             if vector_runs:
-                for q in range(TENSOR_ONLY_BANKS):
-                    quantise(r, q)
                 vector_relu(r)
-            if sums:
-                sort_sums(sums)
-            if vector_runs:
-                for q in range(TENSOR_ONLY_BANKS, BANKS):
-                    quantise(r, q)
+                quantise(r, 0)
+                quantise(r, 1)
 
-        product = const.tile([D_OUT, SHIFTS, ROWS], F32)
-        msg = const.tile([D_OUT, SHIFTS, GRAPHS, NODES], F32)
-        for q in range(BANKS):
-            shifts = slice(q * BANK_SHIFTS, (q + 1) * BANK_SHIFTS)
+        product = const.tile([D_OUT, 2 * PART_COLS], F32)
+        msg = const.tile([D_OUT, NODES, GRAPHS, HALVES, HALF], F32)
+        for q in range(2 * PART_BANKS):
+            cols = slice(q * BANK_COLS, (q + 1) * BANK_COLS)
             nc.scalar.activation(
-                out=product[:, shifts, :].rearrange("d s r -> d (s r)"),
-                in_=acc[q][:],
-                func=RELU,
-                bias=mb2_col[:, 0:1],
+                out=product[:, cols], in_=acc[q][:], func=RELU, bias=mb2_col[:, 0:1]
             )
-            if q < TENSOR_ONLY_BANKS:
+            if q < PART_BANKS:
+                terms = slice(q * BANK_COLS // ROWS, (q + 1) * BANK_COLS // ROWS)
                 nc.vector.tensor_tensor(
-                    out=msg[:, shifts, :, :].rearrange("d s b i -> d s (b i)"),
-                    in0=product[:, shifts, :],
-                    in1=mask_cols[:, shifts, :, :].rearrange("d s b i -> d s (b i)"),
+                    out=msg[:, terms, :, :, :].rearrange("d m b h i -> d (m b h i)"),
+                    in0=product[:, cols],
+                    in1=mask_cross[:, terms, :, :].rearrange("d m n i -> d (m n i)"),
                     op=MULT,
                 )
-        product_vector = product[:, TENSOR_SHIFTS:SHIFTS, :].rearrange("d s r -> d (s r)")
-        plain_col = PLAIN_FIRST // PACK
-        nc.vector.tensor_tensor(
-            out=msg[:, TENSOR_SHIFTS:SHIFTS, 1:GRAPHS, :],
-            in0=product_vector[:, 0:plain_col].rearrange(
-                "d (s b i) -> d s b i", s=VECTOR_SHIFTS, b=GRAPHS - 1
-            ),
-            in1=mask_cols[:, TENSOR_SHIFTS:SHIFTS, 1:GRAPHS, :],
-            op=MULT,
-        )
-        nc.vector.tensor_tensor(
-            out=msg[:, TENSOR_SHIFTS:SHIFTS, 0, :],
-            in0=product_vector[:, plain_col:].rearrange("d (s i) -> d s i", s=VECTOR_SHIFTS),
-            in1=mask_cols[:, TENSOR_SHIFTS:SHIFTS, 0, :],
-            op=MULT,
-        )
+        same = product[:, PART_COLS:]
+        for half in range(HALVES):
+            shape = [D_OUT, HALF, VECTOR_GRAPHS, HALF]
+            nc.vector.tensor_tensor(
+                out=msg[:, HALF:NODES, PLAIN_GRAPHS:, half, :],
+                in0=same[:, half * HALF_COLS : (half + 1) * HALF_COLS].rearrange(
+                    "d (j b i) -> d j b i", j=HALF, b=VECTOR_GRAPHS
+                ),
+                in1=mask_same[:, half, :, PLAIN_GRAPHS:].unsqueeze(3).to_broadcast(shape),
+                op=MULT,
+            )
+            nc.vector.tensor_tensor(
+                out=msg[:, HALF:NODES, 0, half, :],
+                in0=same[:, VECTOR_COLS + half * HALF * HALF : VECTOR_COLS + (half + 1) * HALF * HALF]
+                .rearrange("d (j i) -> d j i", j=HALF),
+                in1=mask_same[:, half, :, 0:1].to_broadcast([D_OUT, HALF, HALF]),
+                op=MULT,
+            )
         out_bank = work_banks.tile([ROWS, D_OUT], F32, tag="bank")
-        for s in range(SHIFTS):
+        for m in range(NODES):
             nc.tensor.matmul(
                 out_bank[:],
-                lhsT=msg[:, s, :, :].rearrange("d b i -> d (b i)"),
+                lhsT=msg[:, m, :, :, :].rearrange("d b h i -> d (b h i)"),
                 rhs=ident[:],
-                start=(s == 0),
-                stop=(s == SHIFTS - 1),
+                start=(m == 0),
+                stop=(m == NODES - 1),
                 is_transpose=True,
             )
         out_sb = const.tile([ROWS, D_OUT], F32)

@@ -35,16 +35,13 @@ LOAD_COLS = LOAD_PASSES * K_PASS
 WEIGHT_LOAD_PASSES = 8
 
 VECTOR_GRAPHS = GRAPHS - 1
-HALF_COLS = HALF * VECTOR_GRAPHS * HALF
+HALF_COLS = HALF * HALF * VECTOR_GRAPHS
 VECTOR_COLS = HALVES * HALF_COLS
 PLAIN_GRAPHS = 1
 LAST_PLAIN_GRAPHS = 3
 PLAIN_XJ_ROW = LAST_PLAIN_GRAPHS * NODES
 PLAIN_MB1_ROW = 2 * LAST_PLAIN_GRAPHS * NODES
 PLAIN_RING = 3
-SCALAR_RELU_SENDERS = 4
-SCALAR_RELU_COLS = SCALAR_RELU_SENDERS * VECTOR_GRAPHS * HALF
-SCALAR_RELU_PLACE = 2
 
 FLOPS = 2 * GRAPHS * NODES * NODES * HIDDEN * D_OUT
 
@@ -147,7 +144,7 @@ def tile_graphdynamics_pa_k_kernel(
             xi_planes = planes[g][0]
             xi_bank = work_banks.tile([P, PACK, ROWS], F32, tag="bank")
             for t in range(PACK):
-                nc.tensor.transpose(xi_bank[:, t, :], xi_planes[:, t, :], by_half[:])
+                nc.tensor.transpose(xi_bank[:, t, :], xi_planes[:, t, :], by_node[:])
             xj_words = rows_of_pass(g)[2].bitcast(F32)
             xj_bank = work_banks.tile([P, PACK // 2, ROWS], F32, tag="bank")
             for u in range(PACK // 2):
@@ -155,8 +152,8 @@ def tile_graphdynamics_pa_k_kernel(
             xi_t = turned.tile([P, HALVES * VECTOR_GRAPHS * HALF * PACK], F32)
             xi_view = xi_t[:, 0 : HALVES * graphs * HALF * PACK]
             nc.scalar.copy(
-                out=xi_view.rearrange("p (h c t) -> p h c t", h=HALVES, t=PACK),
-                in_=xi_bank[:].rearrange("p t (h c) -> p h c t", h=HALVES)[:, :, first * HALF :, :],
+                out=xi_view.rearrange("p (n b t) -> p n b t", n=NODES, t=PACK),
+                in_=xi_bank[:].rearrange("p t (n b) -> p n b t", n=NODES)[:, :, first:, :],
             )
             xj_t = turned.tile([P, NODES * VECTOR_GRAPHS * PACK], BF16)
             xj_view = xj_t[:, 0 : NODES * graphs * PACK]
@@ -165,7 +162,7 @@ def tile_graphdynamics_pa_k_kernel(
                 in_=xj_bank[:].rearrange("p u (b j) -> p j b u", b=GRAPHS)[:, :, first:, :],
             )
             operands[g] = (
-                xi_view.rearrange("p (h b i t) -> p h b i t", h=HALVES, b=graphs, t=PACK),
+                xi_view.rearrange("p (i b t) -> p i b t", i=NODES, b=graphs),
                 xj_view.rearrange("p (j b t) -> p j b t", j=NODES, b=graphs),
             )
 
@@ -184,23 +181,19 @@ def tile_graphdynamics_pa_k_kernel(
                         stop=True,
                     )
                 if b == 0:
-                    h_graph = h_same[:, VECTOR_COLS * PACK :].rearrange(
-                        "p (n c) -> p n c", n=NODES
-                    )
+                    h_graph = h_same[:, VECTOR_COLS * PACK :].rearrange("p (c t) -> p c t", t=PACK)
                 else:
                     h_graph = h_same[:, 0 : VECTOR_COLS * PACK].rearrange(
-                        "p (n b c) -> p n b c", n=NODES, b=VECTOR_GRAPHS
+                        "p (c b t) -> p c b t", b=VECTOR_GRAPHS, t=PACK
                     )[:, :, b - 1, :]
                 nc.scalar.activation(
-                    out=h_graph.rearrange("p n (i t) -> p n i t", t=PACK),
-                    in_=bank[:].rearrange("p t (n i) -> p n i t", n=NODES),
-                    func=RELU,
+                    out=h_graph, in_=bank[:].rearrange("p t c -> p c t"), func=RELU
                 )
 
-        def tensor_line(g, first, end):
+        def tensor_line(g):
             xi_planes, xj_planes = planes[g]
             h_cross = h_tiles[g][0]
-            for d in range(first, end):
+            for d in range(HALF):
                 sum_bank = work_banks.tile([P, PACK, ROWS], F32, tag="bank")
                 for t in range(PACK):
                     nc.tensor.matmul(
@@ -230,24 +223,21 @@ def tile_graphdynamics_pa_k_kernel(
         def vector_line_adds(g):
             xi_t, xj_t = operands[g]
             first = plain_graphs(g)
-            shape = [P, HALF, GRAPHS - first, HALF, PACK]
+            shape = [P, HALF, HALF, GRAPHS - first, PACK]
             for half in range(HALVES):
+                nodes = slice(half * HALF, (half + 1) * HALF)
                 h_half = h_tiles[g][1][:, half * HALF_COLS * PACK : (half + 1) * HALF_COLS * PACK]
                 nc.vector.tensor_tensor(
-                    out=h_half.rearrange("p (j b i t) -> p j b i t", j=HALF, b=VECTOR_GRAPHS, t=PACK)[
-                        :, :, first - 1 :, :, :
+                    out=h_half.rearrange("p (j i b t) -> p j i b t", j=HALF, i=HALF, t=PACK)[
+                        :, :, :, first - 1 :, :
                     ],
-                    in0=xi_t[:, half, :, :, :].unsqueeze(1).to_broadcast(shape),
-                    in1=xj_t[:, half * HALF : (half + 1) * HALF, :, :].unsqueeze(3).to_broadcast(shape),
+                    in0=xi_t[:, nodes, :, :].unsqueeze(1).to_broadcast(shape),
+                    in1=xj_t[:, nodes, :, :].unsqueeze(2).to_broadcast(shape),
                     op=ADD,
                 )
 
-        def scalar_relu(g):
-            h_scalar = h_tiles[g][1][:, 0 : SCALAR_RELU_COLS * PACK]
-            nc.scalar.activation(out=h_scalar, in_=h_scalar, func=RELU)
-
         def vector_relu(g):
-            h_vector = h_tiles[g][1][:, SCALAR_RELU_COLS * PACK : VECTOR_COLS * PACK]
+            h_vector = h_tiles[g][1][:, 0 : VECTOR_COLS * PACK]
             nc.vector.tensor_scalar_max(out=h_vector, in0=h_vector, scalar1=0.0)
 
         def quantise(g, part):
@@ -308,10 +298,10 @@ def tile_graphdynamics_pa_k_kernel(
                 .bitcast(I32),
             )
 
-        by_half = const.tile([P, P], F32)
+        by_node = const.tile([P, P], F32)
         nc.vector.tensor_copy(
-            out=by_half[:].rearrange("k (h b i) -> k h b i", h=HALVES, b=GRAPHS),
-            in_=ident[:].rearrange("k (b h i) -> k h b i", h=HALVES, b=GRAPHS),
+            out=by_node[:].rearrange("k (n b) -> k n b", b=GRAPHS),
+            in_=ident[:].rearrange("k (b n) -> k n b", b=GRAPHS),
         )
         cross_perm = const.tile([ROWS, HALF, GRAPHS * HALVES, HALF], F32)
         swap_halves(
@@ -380,13 +370,9 @@ def tile_graphdynamics_pa_k_kernel(
                 if r >= 0:
                     plain_line(r + 1)
                 turn_operands(r + 1)
-                tensor_line(r + 1, 0, SCALAR_RELU_PLACE)
+                tensor_line(r + 1)
                 if r < 0:
                     plain_line(r + 1)
-            if vector_runs:
-                scalar_relu(r)
-            if tensor_runs:
-                tensor_line(r + 1, SCALAR_RELU_PLACE, HALF)
             if sort_runs:
                 sort_receivers(r + 2)
             if vector_runs:
@@ -415,7 +401,7 @@ def tile_graphdynamics_pa_k_kernel(
             nc.vector.tensor_tensor(
                 out=msg[:, HALF:NODES, PLAIN_GRAPHS:, half, :],
                 in0=same[:, half * HALF_COLS : (half + 1) * HALF_COLS].rearrange(
-                    "d (j b i) -> d j b i", j=HALF, b=VECTOR_GRAPHS
+                    "d (j i b) -> d j b i", j=HALF, b=VECTOR_GRAPHS
                 ),
                 in1=mask_same[:, half, :, PLAIN_GRAPHS:].unsqueeze(3).to_broadcast(shape),
                 op=MULT,

@@ -27,6 +27,8 @@ PASSES = HIDDEN // K_PASS
 PART_COLS = HALF * ROWS
 BANK_COLS = 512
 PART_BANKS = PART_COLS // BANK_COLS
+BANK_ORDER = [2, 3, 0, 1]
+LAST_TERMS = 2
 QUADRANT = 32
 QUADRANT_SCALES = 4
 LOAD_PASSES = 4
@@ -37,17 +39,16 @@ WEIGHT_LOAD_PASSES = 8
 VECTOR_GRAPHS = GRAPHS - 1
 HALF_COLS = HALF * HALF * VECTOR_GRAPHS
 VECTOR_COLS = HALVES * HALF_COLS
-PLAIN_GRAPHS = 1
-LAST_PLAIN_GRAPHS = 3
-PLAIN_XJ_ROW = LAST_PLAIN_GRAPHS * NODES
-PLAIN_MB1_ROW = 2 * LAST_PLAIN_GRAPHS * NODES
+PLAIN_XJ_ROW = NODES
+PLAIN_MB1_ROW = 2 * NODES
 PLAIN_RING = 3
+SCALAR_RELU_SENDERS = 4
+SCALAR_RELU_COLS = SCALAR_RELU_SENDERS * HALF * VECTOR_GRAPHS
+SCALAR_RELU_PLACES = (3, 6)
+SCALAR_RELU_PIECE = SCALAR_RELU_COLS // len(SCALAR_RELU_PLACES)
+SORT_PASSES = 2
 
 FLOPS = 2 * GRAPHS * NODES * NODES * HIDDEN * D_OUT
-
-
-def plain_graphs(g):
-    return LAST_PLAIN_GRAPHS if g == PASSES - 1 else PLAIN_GRAPHS
 
 
 def rotate_in_halves(copy, dst, src, d):
@@ -72,7 +73,8 @@ def tile_graphdynamics_pa_k_kernel(
     with ExitStack() as stack:
         const = stack.enter_context(tc.tile_pool(name="const", bufs=1))
         loads = stack.enter_context(tc.tile_pool(name="loads", bufs=3))
-        sorted_rows = stack.enter_context(tc.tile_pool(name="sorted_rows", bufs=3))
+        sorted_senders = stack.enter_context(tc.tile_pool(name="sorted_senders", bufs=4))
+        sorted_receivers = stack.enter_context(tc.tile_pool(name="sorted_receivers", bufs=3))
         turned = stack.enter_context(tc.tile_pool(name="turned", bufs=2))
         hidden = stack.enter_context(tc.tile_pool(name="hidden", bufs=3))
         quantised = stack.enter_context(tc.tile_pool(name="quantised", bufs=3))
@@ -81,9 +83,11 @@ def tile_graphdynamics_pa_k_kernel(
         stack.enter_context(tc.manual_schedule())
 
         loaded = {}
-        planes = {}
+        sender_planes = {}
+        receiver_planes = {}
         operands = {}
-        h_tiles = {}
+        h_cross = {}
+        h_same = {}
         mx_tiles = {}
 
         def load_rows(c, cuts):
@@ -112,88 +116,80 @@ def tile_graphdynamics_pa_k_kernel(
                 in_=mb1[k_cols].rearrange("(o k) -> o k", o=1),
             )
 
-        def rows_of_pass(g):
-            cols = slice((g % LOAD_PASSES) * K_PASS, (g % LOAD_PASSES + 1) * K_PASS)
-            xi_nat, mb1_nat, xj_nat = loaded[g // LOAD_PASSES]
-            return xi_nat[:, cols], mb1_nat[:, cols], xj_nat[:, cols]
+        def senders_of_pass(g):
+            return loaded[g // LOAD_PASSES][2][
+                :, g % LOAD_PASSES * K_PASS : (g % LOAD_PASSES + 1) * K_PASS
+            ]
 
         def sort_senders(g):
             if g % LOAD_PASSES == 0 and g // LOAD_PASSES + 1 < LOADS:
                 load_rows(g // LOAD_PASSES + 1, cuts=1)
                 load_plain_rows(g // LOAD_PASSES + 1)
-            xi_planes = sorted_rows.tile([ROWS, PACK, P], F32)
-            xj_planes = sorted_rows.tile([ROWS, PACK, P], F32)
-            planes[g] = (xi_planes, xj_planes)
+            xj_planes = sorted_senders.tile([ROWS, PACK, P], F32)
+            sender_planes[g] = xj_planes
             nc.scalar.copy(
                 out=xj_planes[:].rearrange("r t p -> r p t"),
-                in_=rows_of_pass(g)[2].rearrange("r (p t) -> r p t", t=PACK),
+                in_=senders_of_pass(g).rearrange("r (p t) -> r p t", t=PACK),
             )
 
-        def sort_receivers(g):
-            xi_bf16, mb1_bf16, xj_bf16 = rows_of_pass(g)
+        def sort_receivers(g, passes):
+            xi_planes = sorted_receivers.tile([ROWS, SORT_PASSES, PACK, P], F32)
+            for n in range(passes):
+                receiver_planes[g + n] = xi_planes[:, n, :, :]
+            xi_nat, mb1_nat, xj_nat = loaded[g // LOAD_PASSES]
+            cols = slice(g % LOAD_PASSES * K_PASS, (g % LOAD_PASSES + passes) * K_PASS)
             nc.vector.tensor_tensor(
-                out=planes[g][0][:].rearrange("r t p -> r p t"),
-                in0=xi_bf16.rearrange("r (p t) -> r p t", t=PACK),
-                in1=mb1_bf16.rearrange("r (p t) -> r p t", t=PACK),
+                out=xi_planes[:, 0:passes, :, :].rearrange("r n t p -> r n p t"),
+                in0=xi_nat[:, cols].rearrange("r (n p t) -> r n p t", p=P, t=PACK),
+                in1=mb1_nat[:, cols].rearrange("r (n p t) -> r n p t", p=P, t=PACK),
                 op=ADD,
             )
 
         def turn_operands(g):
-            first = plain_graphs(g)
-            graphs = GRAPHS - first
-            xi_planes = planes[g][0]
+            xi_planes = receiver_planes[g]
             xi_bank = work_banks.tile([P, PACK, ROWS], F32, tag="bank")
             for t in range(PACK):
                 nc.tensor.transpose(xi_bank[:, t, :], xi_planes[:, t, :], by_node[:])
-            xj_words = rows_of_pass(g)[2].bitcast(F32)
+            xj_words = senders_of_pass(g).bitcast(F32)
             xj_bank = work_banks.tile([P, PACK // 2, ROWS], F32, tag="bank")
             for u in range(PACK // 2):
                 nc.tensor.transpose(xj_bank[:, u, :], xj_words[:, u : K_PASS // 2 : 2], ident[:])
-            xi_t = turned.tile([P, HALVES * VECTOR_GRAPHS * HALF * PACK], F32)
-            xi_view = xi_t[:, 0 : HALVES * graphs * HALF * PACK]
+            xi_t = turned.tile([P, NODES, VECTOR_GRAPHS, PACK], F32)
             nc.scalar.copy(
-                out=xi_view.rearrange("p (n b t) -> p n b t", n=NODES, t=PACK),
-                in_=xi_bank[:].rearrange("p t (n b) -> p n b t", n=NODES)[:, :, first:, :],
+                out=xi_t[:],
+                in_=xi_bank[:].rearrange("p t (n b) -> p n b t", n=NODES)[:, :, 1:, :],
             )
-            xj_t = turned.tile([P, NODES * VECTOR_GRAPHS * PACK], BF16)
-            xj_view = xj_t[:, 0 : NODES * graphs * PACK]
+            xj_t = turned.tile([P, NODES, VECTOR_GRAPHS, PACK], BF16)
             nc.scalar.copy(
-                out=xj_view.bitcast(F32).rearrange("p (j b u) -> p j b u", j=NODES, b=graphs),
-                in_=xj_bank[:].rearrange("p u (b j) -> p j b u", b=GRAPHS)[:, :, first:, :],
+                out=xj_t[:]
+                .rearrange("p j b t -> p (j b t)")
+                .bitcast(F32)
+                .rearrange("p (j b u) -> p j b u", j=NODES, b=VECTOR_GRAPHS),
+                in_=xj_bank[:].rearrange("p u (b j) -> p j b u", b=GRAPHS)[:, :, 1:, :],
             )
-            operands[g] = (
-                xi_view.rearrange("p (i b t) -> p i b t", i=NODES, b=graphs),
-                xj_view.rearrange("p (j b t) -> p j b t", j=NODES, b=graphs),
-            )
+            operands[g] = (xi_t, xj_t)
 
         def plain_line(g):
             rows = plain_rows[g // LOAD_PASSES % PLAIN_RING]
             k_first = g % LOAD_PASSES * K_PASS
-            h_same = h_tiles[g][1]
-            for b in range(plain_graphs(g)):
-                bank = work_banks.tile([P, PACK, ROWS], F32, tag="bank")
-                for t in range(PACK):
-                    nc.tensor.matmul(
-                        bank[:, t, :],
-                        lhsT=rows[:, k_first + t : k_first + K_PASS : PACK],
-                        rhs=plain_select[:, b, :, :, :].rearrange("k h j i -> k (h j i)"),
-                        start=True,
-                        stop=True,
-                    )
-                if b == 0:
-                    h_graph = h_same[:, VECTOR_COLS * PACK :].rearrange("p (c t) -> p c t", t=PACK)
-                else:
-                    h_graph = h_same[:, 0 : VECTOR_COLS * PACK].rearrange(
-                        "p (c b t) -> p c b t", b=VECTOR_GRAPHS, t=PACK
-                    )[:, :, b - 1, :]
-                nc.scalar.activation(
-                    out=h_graph, in_=bank[:].rearrange("p t c -> p c t"), func=RELU
+            bank = work_banks.tile([P, PACK, ROWS], F32, tag="bank")
+            for t in range(PACK):
+                nc.tensor.matmul(
+                    bank[:, t, :],
+                    lhsT=rows[:, k_first + t : k_first + K_PASS : PACK],
+                    rhs=plain_select[:].rearrange("k h j i -> k (h j i)"),
+                    start=True,
+                    stop=True,
                 )
+            nc.scalar.activation(
+                out=h_same[g][:, VECTOR_COLS * PACK :].rearrange("p (c t) -> p c t", t=PACK),
+                in_=bank[:].rearrange("p t c -> p c t"),
+                func=RELU,
+            )
 
-        def tensor_line(g):
-            xi_planes, xj_planes = planes[g]
-            h_cross = h_tiles[g][0]
-            for d in range(HALF):
+        def tensor_line(g, first, end):
+            xi_planes, xj_planes = receiver_planes[g], sender_planes[g]
+            for d in range(first, end):
                 sum_bank = work_banks.tile([P, PACK, ROWS], F32, tag="bank")
                 for t in range(PACK):
                     nc.tensor.matmul(
@@ -213,7 +209,7 @@ def tile_graphdynamics_pa_k_kernel(
                         is_transpose=True,
                     )
                 nc.scalar.activation(
-                    out=h_cross[:, d * ROWS * PACK : (d + 1) * ROWS * PACK].rearrange(
+                    out=h_cross[g][:, d * ROWS * PACK : (d + 1) * ROWS * PACK].rearrange(
                         "p (r t) -> p r t", t=PACK
                     ),
                     in_=sum_bank[:].rearrange("p t r -> p r t"),
@@ -222,34 +218,48 @@ def tile_graphdynamics_pa_k_kernel(
 
         def vector_line_adds(g):
             xi_t, xj_t = operands[g]
-            first = plain_graphs(g)
-            shape = [P, HALF, HALF, GRAPHS - first, PACK]
-            for half in range(HALVES):
-                nodes = slice(half * HALF, (half + 1) * HALF)
-                h_half = h_tiles[g][1][:, half * HALF_COLS * PACK : (half + 1) * HALF_COLS * PACK]
-                nc.vector.tensor_tensor(
-                    out=h_half.rearrange("p (j i b t) -> p j i b t", j=HALF, i=HALF, t=PACK)[
-                        :, :, :, first - 1 :, :
-                    ],
-                    in0=xi_t[:, nodes, :, :].unsqueeze(1).to_broadcast(shape),
-                    in1=xj_t[:, nodes, :, :].unsqueeze(2).to_broadcast(shape),
-                    op=ADD,
-                )
+            shape = [P, HALVES, HALF, HALF, VECTOR_GRAPHS, PACK]
+            nc.vector.tensor_tensor(
+                out=h_same[g][:, 0 : VECTOR_COLS * PACK].rearrange(
+                    "p (h j i b t) -> p h j i b t", h=HALVES, j=HALF, i=HALF, t=PACK
+                ),
+                in0=xi_t[:]
+                .rearrange("p (h i) b t -> p h i b t", h=HALVES)
+                .unsqueeze(2)
+                .to_broadcast(shape),
+                in1=xj_t[:]
+                .rearrange("p (h j) b t -> p h j b t", h=HALVES)
+                .unsqueeze(3)
+                .to_broadcast(shape),
+                op=ADD,
+            )
+
+        def scalar_relu(g, piece):
+            cols = slice(piece * SCALAR_RELU_PIECE * PACK, (piece + 1) * SCALAR_RELU_PIECE * PACK)
+            h_scalar = h_same[g][:, cols]
+            nc.scalar.activation(out=h_scalar, in_=h_scalar, func=RELU)
 
         def vector_relu(g):
-            h_vector = h_tiles[g][1][:, 0 : VECTOR_COLS * PACK]
+            h_vector = h_same[g][:, SCALAR_RELU_COLS * PACK : VECTOR_COLS * PACK]
             nc.vector.tensor_scalar_max(out=h_vector, in0=h_vector, scalar1=0.0)
 
         def quantise(g, part):
+            h = (h_cross, h_same)[part][g]
             h_codes = quantised.tile([P, PART_COLS], U32, align_bytes=64, tag="codes%d" % part)
             h_scales = quantised.tile([P, PART_COLS], U8, align_bytes=64, tag="scales%d" % part)
             mx_tiles[g, part] = (h_codes, h_scales)
-            nc.vector.quantize_mx(
-                out=h_codes[:].bitcast(FP8X4), scales=h_scales[:], in_=h_tiles[g][part][:]
-            )
+            pieces = PART_BANKS if part == 0 and g == PASSES - 1 else 1
+            width = PART_COLS // pieces
+            for piece in range(pieces):
+                cols = slice(piece * width, (piece + 1) * width)
+                nc.vector.quantize_mx(
+                    out=h_codes[:, cols].bitcast(FP8X4),
+                    scales=h_scales[:, cols],
+                    in_=h[:, piece * width * PACK : (piece + 1) * width * PACK],
+                )
 
         def multiply(g):
-            for q in range(2 * PART_BANKS):
+            for q in BANK_ORDER:
                 h_codes, h_scales = mx_tiles[g, q // PART_BANKS]
                 cols = slice(q % PART_BANKS * BANK_COLS, (q % PART_BANKS + 1) * BANK_COLS)
                 nc.tensor.matmul_mx(
@@ -264,13 +274,6 @@ def tile_graphdynamics_pa_k_kernel(
 
         ident = const.tile([P, P], F32)
         make_identity(nc, ident[:])
-        mb2_bf16 = const.tile([D_OUT, 1], BF16)
-        nc.sync.dma_start(out=mb2_bf16[:], in_=mb2.rearrange("(d o) -> d o", o=1))
-        mask_row = const.tile([P, GRAPHS, HALVES, HALF], BF16)
-        nc.sync.dma_start(
-            out=mask_row[:].rearrange("p b h i -> p (b h i)"),
-            in_=node_mask.rearrange("b n -> (b n)").partition_broadcast(P),
-        )
         plain_rows = []
         for i in range(PLAIN_RING):
             rows = const.tile([P, LOAD_COLS], BF16, name="plain_rows%d" % i)
@@ -278,6 +281,13 @@ def tile_graphdynamics_pa_k_kernel(
             plain_rows.append(rows)
         load_rows(0, cuts=LOAD_PASSES)
         load_plain_rows(0)
+        mb2_bf16 = const.tile([D_OUT, 1], BF16)
+        nc.sync.dma_start(out=mb2_bf16[:], in_=mb2.rearrange("(d o) -> d o", o=1))
+        mask_row = const.tile([P, GRAPHS, HALVES, HALF], BF16)
+        nc.sync.dma_start(
+            out=mask_row[:].rearrange("p b h i -> p (b h i)"),
+            in_=node_mask.rearrange("b n -> (b n)").partition_broadcast(P),
+        )
         w_words = const.tile([P, PASSES, PACK * D_OUT], U8, align_bytes=64)
         w_scales = const.tile([P, PASSES, D_OUT], U8, align_bytes=64)
         nc.gpsimd.memset(w_scales[:].rearrange("p g n -> p (g n)").bitcast(I32), 0)
@@ -311,28 +321,24 @@ def tile_graphdynamics_pa_k_kernel(
         )
         for d in range(1, HALF):
             rotate_in_halves(nc.vector.tensor_copy, cross_perm[:, d, :, :], cross_perm[:, 0, :, :], d)
-        plain_select = const.tile([P, LAST_PLAIN_GRAPHS, HALVES, HALF, HALF], BF16)
+        plain_select = const.tile([P, HALVES, HALF, HALF], BF16)
 
         def build_plain_select():
-            for b in range(LAST_PLAIN_GRAPHS):
-                for half in range(HALVES):
-                    xi_first = b * NODES + half * HALF
-                    xj_first = PLAIN_XJ_ROW + xi_first
-                    nc.vector.scalar_tensor_tensor(
-                        out=plain_select[:, b, half, :, :],
-                        in0=ident[:, xi_first : xi_first + HALF]
-                        .unsqueeze(1)
-                        .to_broadcast([P, HALF, HALF]),
-                        scalar=ident[:, PLAIN_MB1_ROW : PLAIN_MB1_ROW + 1],
-                        in1=ident[:, xj_first : xj_first + HALF]
-                        .unsqueeze(2)
-                        .to_broadcast([P, HALF, HALF]),
-                        op0=ADD,
-                        op1=ADD,
-                    )
+            shape = [P, HALF, HALF]
+            for half in range(HALVES):
+                xi_first = half * HALF
+                xj_first = PLAIN_XJ_ROW + half * HALF
+                nc.vector.scalar_tensor_tensor(
+                    out=plain_select[:, half, :, :],
+                    in0=ident[:, xi_first : xi_first + HALF].unsqueeze(1).to_broadcast(shape),
+                    scalar=ident[:, PLAIN_MB1_ROW : PLAIN_MB1_ROW + 1],
+                    in1=ident[:, xj_first : xj_first + HALF].unsqueeze(2).to_broadcast(shape),
+                    op0=ADD,
+                    op1=ADD,
+                )
 
         mb2_col = const.tile([D_OUT, 1], F32)
-        nc.vector.tensor_copy(out=mb2_col[:], in_=mb2_bf16[:])
+        nc.gpsimd.tensor_copy(out=mb2_col[:], in_=mb2_bf16[:])
         mask_cross = const.tile([P, HALF, GRAPHS * HALVES, HALF], F32)
         swap_halves(
             nc.gpsimd.tensor_copy,
@@ -351,59 +357,64 @@ def tile_graphdynamics_pa_k_kernel(
             acc_banks.tile([D_OUT, BANK_COLS], F32, name="acc%d" % q) for q in range(2 * PART_BANKS)
         ]
 
-        for r in range(-2, PASSES + 1):
-            vector_runs = 0 <= r < PASSES
-            tensor_runs = 0 <= r + 1 < PASSES
-            sort_runs = r + 2 < PASSES
-            if vector_runs:
-                vector_line_adds(r)
+        for r in range(-3, PASSES + 1):
+            if 0 <= r + 1 < PASSES:
+                h_same[r + 1] = hidden.tile([P, PART_COLS * PACK], BF16, align_bytes=64, name="same")
+                h_cross[r + 1] = hidden.tile([P, PART_COLS * PACK], BF16, align_bytes=64, name="cross")
+                vector_line_adds(r + 1)
             if r >= 1:
                 multiply(r - 1)
-            if sort_runs:
-                sort_senders(r + 2)
-            if r == -1:
+            if r + 3 < PASSES:
+                sort_senders(r + 3)
+            if r == -2:
                 build_plain_select()
-            if tensor_runs:
-                h_cross = hidden.tile([P, PART_COLS * PACK], BF16, align_bytes=64)
-                h_same = hidden.tile([P, PART_COLS * PACK], BF16, align_bytes=64)
-                h_tiles[r + 1] = (h_cross, h_same)
-                if r >= 0:
-                    plain_line(r + 1)
-                turn_operands(r + 1)
-                tensor_line(r + 1)
-                if r < 0:
-                    plain_line(r + 1)
-            if sort_runs:
-                sort_receivers(r + 2)
-            if vector_runs:
-                vector_relu(r)
-                quantise(r, 0)
+            if 0 <= r and r + 1 < PASSES:
+                plain_line(r + 1)
+            if 0 <= r + 2 < PASSES:
+                turn_operands(r + 2)
+            if 0 <= r + 1 < PASSES:
+                first = 0
+                for piece, place in enumerate(SCALAR_RELU_PLACES):
+                    tensor_line(r + 1, first, place)
+                    scalar_relu(r + 1, piece)
+                    first = place
+                tensor_line(r + 1, first, HALF)
+            if r == -1:
+                plain_line(r + 1)
+            if r + 3 < SORT_PASSES:
+                sort_receivers(r + 3, 1)
+            elif r + 3 < PASSES and (r + 3) % SORT_PASSES == 0:
+                sort_receivers(r + 3, SORT_PASSES)
+            if 0 <= r < PASSES:
                 quantise(r, 1)
+                quantise(r, 0)
+            if 0 <= r + 1 < PASSES:
+                vector_relu(r + 1)
 
         product = const.tile([D_OUT, 2 * PART_COLS], F32)
         msg = const.tile([D_OUT, NODES, GRAPHS, HALVES, HALF], F32)
-        for q in range(2 * PART_BANKS):
-            cols = slice(q * BANK_COLS, (q + 1) * BANK_COLS)
+
+        def finish(cols):
+            first = cols.start % BANK_COLS
+            bank = acc[cols.start // BANK_COLS]
             nc.scalar.activation(
-                out=product[:, cols], in_=acc[q][:], func=RELU, bias=mb2_col[:, 0:1]
+                out=product[:, cols],
+                in_=bank[:, first : first + cols.stop - cols.start],
+                func=RELU,
+                bias=mb2_col[:, 0:1],
             )
-            if q < PART_BANKS:
-                terms = slice(q * BANK_COLS // ROWS, (q + 1) * BANK_COLS // ROWS)
-                nc.vector.tensor_tensor(
-                    out=msg[:, terms, :, :, :].rearrange("d m b h i -> d (m b h i)"),
-                    in0=product[:, cols],
-                    in1=mask_cross[:, terms, :, :].rearrange("d m n i -> d (m n i)"),
-                    op=MULT,
-                )
+
+        for q in range(PART_BANKS, 2 * PART_BANKS):
+            finish(slice(q * BANK_COLS, (q + 1) * BANK_COLS))
         same = product[:, PART_COLS:]
         for half in range(HALVES):
             shape = [D_OUT, HALF, VECTOR_GRAPHS, HALF]
             nc.vector.tensor_tensor(
-                out=msg[:, HALF:NODES, PLAIN_GRAPHS:, half, :],
+                out=msg[:, HALF:NODES, 1:, half, :],
                 in0=same[:, half * HALF_COLS : (half + 1) * HALF_COLS].rearrange(
                     "d (j i b) -> d j b i", j=HALF, b=VECTOR_GRAPHS
                 ),
-                in1=mask_same[:, half, :, PLAIN_GRAPHS:].unsqueeze(3).to_broadcast(shape),
+                in1=mask_same[:, half, :, 1:].unsqueeze(3).to_broadcast(shape),
                 op=MULT,
             )
             nc.vector.tensor_tensor(
@@ -413,14 +424,25 @@ def tile_graphdynamics_pa_k_kernel(
                 in1=mask_same[:, half, :, 0:1].to_broadcast([D_OUT, HALF, HALF]),
                 op=MULT,
             )
+        for first in range(0, HALF, LAST_TERMS):
+            cols = slice(first * ROWS, (first + LAST_TERMS) * ROWS)
+            terms = slice(first, first + LAST_TERMS)
+            finish(cols)
+            nc.vector.tensor_tensor(
+                out=msg[:, terms, :, :, :].rearrange("d m b h i -> d (m b h i)"),
+                in0=product[:, cols],
+                in1=mask_cross[:, terms, :, :].rearrange("d m n i -> d (m n i)"),
+                op=MULT,
+            )
         out_bank = work_banks.tile([ROWS, D_OUT], F32, tag="bank")
-        for m in range(NODES):
+        for n in range(NODES):
+            m = (HALF + n) % NODES
             nc.tensor.matmul(
                 out_bank[:],
                 lhsT=msg[:, m, :, :, :].rearrange("d b h i -> d (b h i)"),
                 rhs=ident[:],
-                start=(m == 0),
-                stop=(m == NODES - 1),
+                start=(n == 0),
+                stop=(n == NODES - 1),
                 is_transpose=True,
             )
         out_sb = const.tile([ROWS, D_OUT], F32)

@@ -28,7 +28,6 @@ PART_COLS = HALF * ROWS
 BANK_COLS = 512
 PART_BANKS = PART_COLS // BANK_COLS
 BANK_ORDER = [2, 3, 0, 1]
-LAST_TERMS = 2
 QUADRANT = 32
 QUADRANT_SCALES = 4
 LOAD_PASSES = 4
@@ -42,10 +41,7 @@ VECTOR_COLS = HALVES * HALF_COLS
 PLAIN_XJ_ROW = NODES
 PLAIN_MB1_ROW = 2 * NODES
 PLAIN_RING = 3
-SCALAR_RELU_SENDERS = 4
-SCALAR_RELU_COLS = SCALAR_RELU_SENDERS * HALF * VECTOR_GRAPHS
-SCALAR_RELU_PLACES = (3, 6)
-SCALAR_RELU_PIECE = SCALAR_RELU_COLS // len(SCALAR_RELU_PLACES)
+WORDS_PLACE = 4
 SORT_PASSES = 2
 
 FLOPS = 2 * GRAPHS * NODES * NODES * HIDDEN * D_OUT
@@ -84,6 +80,7 @@ def tile_graphdynamics_pa_k_kernel(
 
         loaded = {}
         sender_planes = {}
+        sender_words = {}
         receiver_planes = {}
         operands = {}
         h_cross = {}
@@ -145,15 +142,23 @@ def tile_graphdynamics_pa_k_kernel(
                 op=ADD,
             )
 
+        def sort_words(g):
+            xj_words = sorted_senders.tile([ROWS, PACK // 2, P], F32)
+            sender_words[g] = xj_words
+            nc.scalar.copy(
+                out=xj_words[:].rearrange("r u p -> r p u"),
+                in_=senders_of_pass(g).bitcast(F32).rearrange("r (p u) -> r p u", u=PACK // 2),
+            )
+
         def turn_operands(g):
             xi_planes = receiver_planes[g]
             xi_bank = work_banks.tile([P, PACK, ROWS], F32, tag="bank")
             for t in range(PACK):
                 nc.tensor.transpose(xi_bank[:, t, :], xi_planes[:, t, :], by_node[:])
-            xj_words = senders_of_pass(g).bitcast(F32)
+            xj_words = sender_words[g]
             xj_bank = work_banks.tile([P, PACK // 2, ROWS], F32, tag="bank")
             for u in range(PACK // 2):
-                nc.tensor.transpose(xj_bank[:, u, :], xj_words[:, u : K_PASS // 2 : 2], ident[:])
+                nc.tensor.transpose(xj_bank[:, u, :], xj_words[:, u, :], ident[:])
             xi_t = turned.tile([P, NODES, VECTOR_GRAPHS, PACK], F32)
             nc.scalar.copy(
                 out=xi_t[:],
@@ -234,13 +239,8 @@ def tile_graphdynamics_pa_k_kernel(
                 op=ADD,
             )
 
-        def scalar_relu(g, piece):
-            cols = slice(piece * SCALAR_RELU_PIECE * PACK, (piece + 1) * SCALAR_RELU_PIECE * PACK)
-            h_scalar = h_same[g][:, cols]
-            nc.scalar.activation(out=h_scalar, in_=h_scalar, func=RELU)
-
         def vector_relu(g):
-            h_vector = h_same[g][:, SCALAR_RELU_COLS * PACK : VECTOR_COLS * PACK]
+            h_vector = h_same[g][:, 0 : VECTOR_COLS * PACK]
             nc.vector.tensor_scalar_max(out=h_vector, in0=h_vector, scalar1=0.0)
 
         def quantise(g, part):
@@ -362,23 +362,24 @@ def tile_graphdynamics_pa_k_kernel(
                 h_same[r + 1] = hidden.tile([P, PART_COLS * PACK], BF16, align_bytes=64, name="same")
                 h_cross[r + 1] = hidden.tile([P, PART_COLS * PACK], BF16, align_bytes=64, name="cross")
                 vector_line_adds(r + 1)
+            if 0 <= r and r + 1 < PASSES:
+                plain_line(r + 1)
             if r >= 1:
                 multiply(r - 1)
             if r + 3 < PASSES:
                 sort_senders(r + 3)
             if r == -2:
                 build_plain_select()
-            if 0 <= r and r + 1 < PASSES:
-                plain_line(r + 1)
+            if r < 0:
+                sort_words(r + 3)
             if 0 <= r + 2 < PASSES:
                 turn_operands(r + 2)
             if 0 <= r + 1 < PASSES:
-                first = 0
-                for piece, place in enumerate(SCALAR_RELU_PLACES):
-                    tensor_line(r + 1, first, place)
-                    scalar_relu(r + 1, piece)
-                    first = place
-                tensor_line(r + 1, first, HALF)
+                tensor_line(r + 1, 0, WORDS_PLACE)
+            if 0 <= r and r + 3 < PASSES:
+                sort_words(r + 3)
+            if 0 <= r + 1 < PASSES:
+                tensor_line(r + 1, WORDS_PLACE, HALF)
             if r == -1:
                 plain_line(r + 1)
             if r + 3 < SORT_PASSES:
@@ -394,18 +395,16 @@ def tile_graphdynamics_pa_k_kernel(
         product = const.tile([D_OUT, 2 * PART_COLS], F32)
         msg = const.tile([D_OUT, NODES, GRAPHS, HALVES, HALF], F32)
 
-        def finish(cols):
-            first = cols.start % BANK_COLS
-            bank = acc[cols.start // BANK_COLS]
+        def finish_bank(q):
             nc.scalar.activation(
-                out=product[:, cols],
-                in_=bank[:, first : first + cols.stop - cols.start],
+                out=product[:, q * BANK_COLS : (q + 1) * BANK_COLS],
+                in_=acc[q][:],
                 func=RELU,
                 bias=mb2_col[:, 0:1],
             )
 
         for q in range(PART_BANKS, 2 * PART_BANKS):
-            finish(slice(q * BANK_COLS, (q + 1) * BANK_COLS))
+            finish_bank(q)
         same = product[:, PART_COLS:]
         for half in range(HALVES):
             shape = [D_OUT, HALF, VECTOR_GRAPHS, HALF]
@@ -424,13 +423,12 @@ def tile_graphdynamics_pa_k_kernel(
                 in1=mask_same[:, half, :, 0:1].to_broadcast([D_OUT, HALF, HALF]),
                 op=MULT,
             )
-        for first in range(0, HALF, LAST_TERMS):
-            cols = slice(first * ROWS, (first + LAST_TERMS) * ROWS)
-            terms = slice(first, first + LAST_TERMS)
-            finish(cols)
+        for q in range(PART_BANKS):
+            finish_bank(q)
+            terms = slice(q * BANK_COLS // ROWS, (q + 1) * BANK_COLS // ROWS)
             nc.vector.tensor_tensor(
                 out=msg[:, terms, :, :, :].rearrange("d m b h i -> d (m b h i)"),
-                in0=product[:, cols],
+                in0=product[:, q * BANK_COLS : (q + 1) * BANK_COLS],
                 in1=mask_cross[:, terms, :, :].rearrange("d m n i -> d (m n i)"),
                 op=MULT,
             )

@@ -36,15 +36,23 @@ LOAD_COLS = LOAD_PASSES * K_PASS
 WEIGHT_LOAD_PASSES = 8
 
 VECTOR_GRAPHS = GRAPHS - 1
-HALF_COLS = HALF * HALF * VECTOR_GRAPHS
-VECTOR_COLS = HALVES * HALF_COLS
+SENDER_COLS = HALF * VECTOR_GRAPHS
+FIRST_COLS = HALVES * SENDER_COLS
+OTHERS = HALF - 1
+VECTOR_COLS = HALVES * HALF * SENDER_COLS
 PLAIN_XJ_ROW = NODES
 PLAIN_MB1_ROW = 2 * NODES
+FIRST_XI_ROWS = VECTOR_GRAPHS * NODES
+FIRST_MB1_ROW = FIRST_XI_ROWS + HALVES * VECTOR_GRAPHS
 PLAIN_RING = 3
 WORDS_PLACE = 4
 SORT_PASSES = 2
 
 FLOPS = 2 * GRAPHS * NODES * NODES * HIDDEN * D_OUT
+
+
+def first_senders_are_plain(g):
+    return g % 3 == 1
 
 
 def rotate_in_halves(copy, dst, src, d):
@@ -112,6 +120,18 @@ def tile_graphdynamics_pa_k_kernel(
                 out=rows[PLAIN_MB1_ROW : PLAIN_MB1_ROW + 1, :],
                 in_=mb1[k_cols].rearrange("(o k) -> o k", o=1),
             )
+            rows = first_rows[c % PLAIN_RING]
+            nc.sync.dma_start(out=rows[0:FIRST_XI_ROWS, :], in_=xi_rows[NODES:ROWS, k_cols])
+            for half in range(HALVES):
+                row = FIRST_XI_ROWS + half * VECTOR_GRAPHS
+                nc.sync.dma_start(
+                    out=rows[row : row + VECTOR_GRAPHS, :],
+                    in_=xj_rows[NODES + half * HALF : ROWS : NODES, k_cols],
+                )
+            nc.sync.dma_start(
+                out=rows[FIRST_MB1_ROW : FIRST_MB1_ROW + 1, :],
+                in_=mb1[k_cols].rearrange("(o k) -> o k", o=1),
+            )
 
         def senders_of_pass(g):
             return loaded[g // LOAD_PASSES][2][
@@ -158,7 +178,7 @@ def tile_graphdynamics_pa_k_kernel(
             xj_words = sender_words[g]
             xj_bank = work_banks.tile([P, PACK // 2, ROWS], F32, tag="bank")
             for u in range(PACK // 2):
-                nc.tensor.transpose(xj_bank[:, u, :], xj_words[:, u, :], ident[:])
+                nc.tensor.transpose(xj_bank[:, u, :], xj_words[:, u, :], by_sender[:])
             xi_t = turned.tile([P, NODES, VECTOR_GRAPHS, PACK], F32)
             nc.scalar.copy(
                 out=xi_t[:],
@@ -170,27 +190,43 @@ def tile_graphdynamics_pa_k_kernel(
                 .rearrange("p j b t -> p (j b t)")
                 .bitcast(F32)
                 .rearrange("p (j b u) -> p j b u", j=NODES, b=VECTOR_GRAPHS),
-                in_=xj_bank[:].rearrange("p u (b j) -> p j b u", b=GRAPHS)[:, :, 1:, :],
+                in_=xj_bank[:].rearrange("p u (j b) -> p j b u", b=GRAPHS)[:, :, 1:, :],
             )
             operands[g] = (xi_t, xj_t)
 
-        def plain_line(g):
-            rows = plain_rows[g // LOAD_PASSES % PLAIN_RING]
+        def plain_matmuls(g, rows, select, h_cols):
             k_first = g % LOAD_PASSES * K_PASS
+            cols = select.shape[1]
             bank = work_banks.tile([P, PACK, ROWS], F32, tag="bank")
             for t in range(PACK):
                 nc.tensor.matmul(
-                    bank[:, t, :],
+                    bank[:, t, 0:cols],
                     lhsT=rows[:, k_first + t : k_first + K_PASS : PACK],
-                    rhs=plain_select[:].rearrange("k h j i -> k (h j i)"),
+                    rhs=select,
                     start=True,
                     stop=True,
                 )
             nc.scalar.activation(
-                out=h_same[g][:, VECTOR_COLS * PACK :].rearrange("p (c t) -> p c t", t=PACK),
-                in_=bank[:].rearrange("p t c -> p c t"),
+                out=h_cols.rearrange("p (c t) -> p c t", t=PACK),
+                in_=bank[:, :, 0:cols].rearrange("p t c -> p c t"),
                 func=RELU,
             )
+
+        def plain_line(g):
+            ring = g // LOAD_PASSES % PLAIN_RING
+            plain_matmuls(
+                g,
+                plain_rows[ring],
+                plain_select[:].rearrange("k h j i -> k (h j i)"),
+                h_same[g][:, VECTOR_COLS * PACK :],
+            )
+            if first_senders_are_plain(g):
+                plain_matmuls(
+                    g,
+                    first_rows[ring],
+                    first_select[:].rearrange("k h i b -> k (h i b)"),
+                    h_same[g][:, 0 : FIRST_COLS * PACK],
+                )
 
         def tensor_line(g, first, end):
             xi_planes, xj_planes = receiver_planes[g], sender_planes[g]
@@ -223,24 +259,34 @@ def tile_graphdynamics_pa_k_kernel(
 
         def vector_line_adds(g):
             xi_t, xj_t = operands[g]
-            shape = [P, HALVES, HALF, HALF, VECTOR_GRAPHS, PACK]
+            receivers = xi_t[:].rearrange("p (h i) b t -> p h i b t", h=HALVES)
+            shape = [P, HALVES, OTHERS, HALF, VECTOR_GRAPHS, PACK]
             nc.vector.tensor_tensor(
-                out=h_same[g][:, 0 : VECTOR_COLS * PACK].rearrange(
-                    "p (h j i b t) -> p h j i b t", h=HALVES, j=HALF, i=HALF, t=PACK
+                out=h_same[g][:, FIRST_COLS * PACK : VECTOR_COLS * PACK].rearrange(
+                    "p (h j i b t) -> p h j i b t", h=HALVES, j=OTHERS, i=HALF, t=PACK
                 ),
-                in0=xi_t[:]
-                .rearrange("p (h i) b t -> p h i b t", h=HALVES)
-                .unsqueeze(2)
-                .to_broadcast(shape),
-                in1=xj_t[:]
+                in0=receivers.unsqueeze(2).to_broadcast(shape),
+                in1=xj_t[:, HALVES:, :, :]
                 .rearrange("p (h j) b t -> p h j b t", h=HALVES)
                 .unsqueeze(3)
                 .to_broadcast(shape),
                 op=ADD,
             )
+            if not first_senders_are_plain(g):
+                nc.vector.tensor_tensor(
+                    out=h_same[g][:, 0 : FIRST_COLS * PACK].rearrange(
+                        "p (h i b t) -> p h i b t", h=HALVES, i=HALF, t=PACK
+                    ),
+                    in0=receivers,
+                    in1=xj_t[:, 0:HALVES, :, :]
+                    .unsqueeze(2)
+                    .to_broadcast([P, HALVES, HALF, VECTOR_GRAPHS, PACK]),
+                    op=ADD,
+                )
 
         def vector_relu(g):
-            h_vector = h_same[g][:, 0 : VECTOR_COLS * PACK]
+            first = FIRST_COLS if first_senders_are_plain(g) else 0
+            h_vector = h_same[g][:, first * PACK : VECTOR_COLS * PACK]
             nc.vector.tensor_scalar_max(out=h_vector, in0=h_vector, scalar1=0.0)
 
         def quantise(g, part):
@@ -275,10 +321,13 @@ def tile_graphdynamics_pa_k_kernel(
         ident = const.tile([P, P], F32)
         make_identity(nc, ident[:])
         plain_rows = []
+        first_rows = []
         for i in range(PLAIN_RING):
-            rows = const.tile([P, LOAD_COLS], BF16, name="plain_rows%d" % i)
-            (nc.vector if i == 0 else nc.gpsimd).memset(rows[:].bitcast(I32), 0)
-            plain_rows.append(rows)
+            for ring, name in ((plain_rows, "plain_rows%d"), (first_rows, "first_rows%d")):
+                rows = const.tile([P, LOAD_COLS], BF16, name=name % i)
+                engine = nc.vector if i == 0 and ring is plain_rows else nc.gpsimd
+                engine.memset(rows[:].bitcast(I32), 0)
+                ring.append(rows)
         load_rows(0, cuts=LOAD_PASSES)
         load_plain_rows(0)
         mb2_bf16 = const.tile([D_OUT, 1], BF16)
@@ -313,6 +362,17 @@ def tile_graphdynamics_pa_k_kernel(
             out=by_node[:].rearrange("k (n b) -> k n b", b=GRAPHS),
             in_=ident[:].rearrange("k (b n) -> k n b", b=GRAPHS),
         )
+        by_sender = const.tile([P, P], F32)
+        nodes = by_node[:].rearrange("k (h j b) -> k h j b", h=HALVES, b=GRAPHS)
+        first_end = HALVES * GRAPHS
+        nc.vector.tensor_copy(
+            out=by_sender[:, 0:first_end].rearrange("k (h b) -> k h b", h=HALVES),
+            in_=nodes[:, :, 0, :],
+        )
+        nc.vector.tensor_copy(
+            out=by_sender[:, first_end:].rearrange("k (h j b) -> k h j b", h=HALVES, b=GRAPHS),
+            in_=nodes[:, :, 1:, :],
+        )
         cross_perm = const.tile([ROWS, HALF, GRAPHS * HALVES, HALF], F32)
         swap_halves(
             nc.vector.tensor_copy,
@@ -323,7 +383,22 @@ def tile_graphdynamics_pa_k_kernel(
             rotate_in_halves(nc.vector.tensor_copy, cross_perm[:, d, :, :], cross_perm[:, 0, :, :], d)
         plain_select = const.tile([P, HALVES, HALF, HALF], BF16)
 
+        first_select = const.tile([P, HALVES, HALF, VECTOR_GRAPHS], BF16)
+
         def build_plain_select():
+            receivers = ident[:, 0:FIRST_XI_ROWS].rearrange("k (b h i) -> k h i b", h=HALVES, i=HALF)
+            for half in range(HALVES):
+                row = FIRST_XI_ROWS + half * VECTOR_GRAPHS
+                nc.vector.scalar_tensor_tensor(
+                    out=first_select[:, half, :, :],
+                    in0=receivers[:, half, :, :],
+                    scalar=ident[:, FIRST_MB1_ROW : FIRST_MB1_ROW + 1],
+                    in1=ident[:, row : row + VECTOR_GRAPHS]
+                    .unsqueeze(1)
+                    .to_broadcast([P, HALF, VECTOR_GRAPHS]),
+                    op0=ADD,
+                    op1=ADD,
+                )
             shape = [P, HALF, HALF]
             for half in range(HALVES):
                 xi_first = half * HALF
@@ -406,14 +481,21 @@ def tile_graphdynamics_pa_k_kernel(
         for q in range(PART_BANKS, 2 * PART_BANKS):
             finish_bank(q)
         same = product[:, PART_COLS:]
+        nc.vector.tensor_tensor(
+            out=msg[:, HALF, 1:, :, :].rearrange("d b h i -> d h b i"),
+            in0=same[:, 0:FIRST_COLS].rearrange("d (h i b) -> d h b i", h=HALVES, i=HALF),
+            in1=mask_same[:, :, 0, 1:].unsqueeze(3).to_broadcast([D_OUT, HALVES, VECTOR_GRAPHS, HALF]),
+            op=MULT,
+        )
         for half in range(HALVES):
-            shape = [D_OUT, HALF, VECTOR_GRAPHS, HALF]
+            col = FIRST_COLS + half * OTHERS * SENDER_COLS
+            shape = [D_OUT, OTHERS, VECTOR_GRAPHS, HALF]
             nc.vector.tensor_tensor(
-                out=msg[:, HALF:NODES, 1:, half, :],
-                in0=same[:, half * HALF_COLS : (half + 1) * HALF_COLS].rearrange(
-                    "d (j i b) -> d j b i", j=HALF, b=VECTOR_GRAPHS
+                out=msg[:, HALF + 1 : NODES, 1:, half, :],
+                in0=same[:, col : col + OTHERS * SENDER_COLS].rearrange(
+                    "d (j i b) -> d j b i", j=OTHERS, b=VECTOR_GRAPHS
                 ),
-                in1=mask_same[:, half, :, 1:].unsqueeze(3).to_broadcast(shape),
+                in1=mask_same[:, half, 1:, 1:].unsqueeze(3).to_broadcast(shape),
                 op=MULT,
             )
             nc.vector.tensor_tensor(

from contextlib import ExitStack

import concourse.mybir as mybir
from concourse.masks import make_identity

F32 = mybir.dt.float32
BF16 = mybir.dt.bfloat16
I32 = mybir.dt.int32
U8 = mybir.dt.uint8
U32 = mybir.dt.uint32
FP8X4 = mybir.dt.float8_e4m3fn_x4
ADD = mybir.AluOpType.add
MULT = mybir.AluOpType.mult
RELU = mybir.ActivationFunctionType.Relu

P = 128
PACK = 4
K_PASS = P * PACK
GRAPHS = 8
NODES = 16
HALVES = 2
HALF = NODES // HALVES
ROWS = GRAPHS * NODES
HIDDEN = 16384
D_OUT = 128
PASSES = HIDDEN // K_PASS
PART_COLS = HALF * ROWS
BANK_COLS = 512
PART_BANKS = PART_COLS // BANK_COLS
BANK_ORDER = [2, 3, 0, 1]
QUADRANT = 32
QUADRANT_SCALES = 4
LOAD_PASSES = 4
LOADS = PASSES // LOAD_PASSES
LOAD_COLS = LOAD_PASSES * K_PASS
WEIGHT_LOAD_PASSES = 8

VECTOR_GRAPHS = GRAPHS - 1
SENDER_COLS = HALF * VECTOR_GRAPHS
FIRST_COLS = HALVES * SENDER_COLS
OTHERS = HALF - 1
VECTOR_COLS = HALVES * HALF * SENDER_COLS
PLAIN_XJ_ROW = NODES
PLAIN_MB1_ROW = 2 * NODES
FIRST_XI_ROWS = VECTOR_GRAPHS * NODES
FIRST_MB1_ROW = FIRST_XI_ROWS + HALVES * VECTOR_GRAPHS
PLAIN_RING = 3
WORDS_PLACE = 4
SORT_PASSES = 2

FLOPS = 2 * GRAPHS * NODES * NODES * HIDDEN * D_OUT


def first_senders_are_plain(g):
    return g % 3 == 1


def rotate_in_halves(copy, dst, src, d):
    copy(out=dst[:, :, 0 : HALF - d], in_=src[:, :, d:HALF])
    if d > 0:
        copy(out=dst[:, :, HALF - d : HALF], in_=src[:, :, 0:d])


def swap_halves(copy, dst, src):
    for half in range(HALVES):
        copy(out=dst[:, :, half, :], in_=src[:, :, 1 - half, :])


def tile_graphdynamics_pa_k_kernel(
    tc, xi_p, xj_p, node_mask, mb1, mw2_words, mw2_scales, mb2, out
):
    nc = tc.nc
    xi_rows = xi_p.rearrange("b n h -> (b n) h")
    xj_rows = xj_p.rearrange("b n h -> (b n) h")
    out_rows = out.rearrange("b n d -> (b n) d")

    with ExitStack() as stack:
        const = stack.enter_context(tc.tile_pool(name="const", bufs=1))
        loads = stack.enter_context(tc.tile_pool(name="loads", bufs=3))
        sorted_senders = stack.enter_context(tc.tile_pool(name="sorted_senders", bufs=4))
        sorted_receivers = stack.enter_context(tc.tile_pool(name="sorted_receivers", bufs=3))
        turned = stack.enter_context(tc.tile_pool(name="turned", bufs=2))
        hidden = stack.enter_context(tc.tile_pool(name="hidden", bufs=3))
        quantised = stack.enter_context(tc.tile_pool(name="quantised", bufs=3))
        acc_banks = stack.enter_context(tc.psum_pool(name="acc_banks", bufs=1))
        work_banks = stack.enter_context(tc.psum_pool(name="work_banks", bufs=4))
        stack.enter_context(tc.manual_schedule())

        loaded = {}
        sender_planes = {}
        sender_words = {}
        receiver_planes = {}
        operands = {}
        h_cross = {}
        h_same = {}
        mx_tiles = {}

        def load_rows(c, cuts):
            xi_nat = loads.tile([ROWS, LOAD_COLS], BF16)
            mb1_nat = loads.tile([ROWS, LOAD_COLS], BF16)
            xj_nat = loads.tile([ROWS, LOAD_COLS], BF16)
            loaded[c] = (xi_nat, mb1_nat, xj_nat)
            width = LOAD_COLS // cuts
            for cut in range(cuts):
                cols = slice(cut * width, (cut + 1) * width)
                k_first = c * LOAD_COLS + cut * width
                k_cols = slice(k_first, k_first + width)
                nc.sync.dma_start(out=xi_nat[:, cols], in_=xi_rows[:, k_cols])
                nc.sync.dma_start(out=mb1_nat[:, cols], in_=mb1[k_cols].partition_broadcast(ROWS))
                nc.sync.dma_start(out=xj_nat[:, cols], in_=xj_rows[:, k_cols])

        def load_plain_rows(c):
            k_cols = slice(c * LOAD_COLS, (c + 1) * LOAD_COLS)
            rows = plain_rows[c % PLAIN_RING]
            nc.sync.dma_start(out=rows[0:PLAIN_XJ_ROW, :], in_=xi_rows[0:PLAIN_XJ_ROW, k_cols])
            nc.sync.dma_start(
                out=rows[PLAIN_XJ_ROW:PLAIN_MB1_ROW, :], in_=xj_rows[0:PLAIN_XJ_ROW, k_cols]
            )
            nc.sync.dma_start(
                out=rows[PLAIN_MB1_ROW : PLAIN_MB1_ROW + 1, :],
                in_=mb1[k_cols].rearrange("(o k) -> o k", o=1),
            )
            rows = first_rows[c % PLAIN_RING]
            nc.sync.dma_start(out=rows[0:FIRST_XI_ROWS, :], in_=xi_rows[NODES:ROWS, k_cols])
            for half in range(HALVES):
                row = FIRST_XI_ROWS + half * VECTOR_GRAPHS
                nc.sync.dma_start(
                    out=rows[row : row + VECTOR_GRAPHS, :],
                    in_=xj_rows[NODES + half * HALF : ROWS : NODES, k_cols],
                )
            nc.sync.dma_start(
                out=rows[FIRST_MB1_ROW : FIRST_MB1_ROW + 1, :],
                in_=mb1[k_cols].rearrange("(o k) -> o k", o=1),
            )

        def senders_of_pass(g):
            return loaded[g // LOAD_PASSES][2][
                :, g % LOAD_PASSES * K_PASS : (g % LOAD_PASSES + 1) * K_PASS
            ]

        def sort_senders(g):
            if g % LOAD_PASSES == 0 and g // LOAD_PASSES + 1 < LOADS:
                load_rows(g // LOAD_PASSES + 1, cuts=1)
                load_plain_rows(g // LOAD_PASSES + 1)
            xj_planes = sorted_senders.tile([ROWS, PACK, P], F32)
            sender_planes[g] = xj_planes
            nc.scalar.copy(
                out=xj_planes[:].rearrange("r t p -> r p t"),
                in_=senders_of_pass(g).rearrange("r (p t) -> r p t", t=PACK),
            )

        def sort_receivers(g, passes):
            xi_planes = sorted_receivers.tile([ROWS, SORT_PASSES, PACK, P], F32)
            for n in range(passes):
                receiver_planes[g + n] = xi_planes[:, n, :, :]
            xi_nat, mb1_nat, xj_nat = loaded[g // LOAD_PASSES]
            cols = slice(g % LOAD_PASSES * K_PASS, (g % LOAD_PASSES + passes) * K_PASS)
            nc.vector.tensor_tensor(
                out=xi_planes[:, 0:passes, :, :].rearrange("r n t p -> r n p t"),
                in0=xi_nat[:, cols].rearrange("r (n p t) -> r n p t", p=P, t=PACK),
                in1=mb1_nat[:, cols].rearrange("r (n p t) -> r n p t", p=P, t=PACK),
                op=ADD,
            )

        def sort_words(g):
            xj_words = sorted_senders.tile([ROWS, PACK // 2, P], F32)
            sender_words[g] = xj_words
            nc.scalar.copy(
                out=xj_words[:].rearrange("r u p -> r p u"),
                in_=senders_of_pass(g).bitcast(F32).rearrange("r (p u) -> r p u", u=PACK // 2),
            )

        def turn_operands(g):
            xi_planes = receiver_planes[g]
            xi_bank = work_banks.tile([P, PACK, ROWS], F32, tag="bank")
            for t in range(PACK):
                nc.tensor.transpose(xi_bank[:, t, :], xi_planes[:, t, :], by_node[:])
            xj_words = sender_words[g]
            xj_bank = work_banks.tile([P, PACK // 2, ROWS], F32, tag="bank")
            for u in range(PACK // 2):
                nc.tensor.transpose(xj_bank[:, u, :], xj_words[:, u, :], by_sender[:])
            xi_t = turned.tile([P, NODES, VECTOR_GRAPHS, PACK], F32)
            nc.scalar.copy(
                out=xi_t[:],
                in_=xi_bank[:].rearrange("p t (n b) -> p n b t", n=NODES)[:, :, 1:, :],
            )
            xj_t = turned.tile([P, NODES, VECTOR_GRAPHS, PACK], BF16)
            nc.scalar.copy(
                out=xj_t[:]
                .rearrange("p j b t -> p (j b t)")
                .bitcast(F32)
                .rearrange("p (j b u) -> p j b u", j=NODES, b=VECTOR_GRAPHS),
                in_=xj_bank[:].rearrange("p u (j b) -> p j b u", b=GRAPHS)[:, :, 1:, :],
            )
            operands[g] = (xi_t, xj_t)

        def plain_matmuls(g, rows, select, h_cols):
            k_first = g % LOAD_PASSES * K_PASS
            cols = select.shape[1]
            bank = work_banks.tile([P, PACK, ROWS], F32, tag="bank")
            for t in range(PACK):
                nc.tensor.matmul(
                    bank[:, t, 0:cols],
                    lhsT=rows[:, k_first + t : k_first + K_PASS : PACK],
                    rhs=select,
                    start=True,
                    stop=True,
                )
            nc.scalar.activation(
                out=h_cols.rearrange("p (c t) -> p c t", t=PACK),
                in_=bank[:, :, 0:cols].rearrange("p t c -> p c t"),
                func=RELU,
            )

        def plain_line(g):
            ring = g // LOAD_PASSES % PLAIN_RING
            plain_matmuls(
                g,
                plain_rows[ring],
                plain_select[:].rearrange("k h j i -> k (h j i)"),
                h_same[g][:, VECTOR_COLS * PACK :],
            )
            if first_senders_are_plain(g):
                plain_matmuls(
                    g,
                    first_rows[ring],
                    first_select[:].rearrange("k h i b -> k (h i b)"),
                    h_same[g][:, 0 : FIRST_COLS * PACK],
                )

        def tensor_line(g, first, end):
            xi_planes, xj_planes = receiver_planes[g], sender_planes[g]
            for d in range(first, end):
                sum_bank = work_banks.tile([P, PACK, ROWS], F32, tag="bank")
                for t in range(PACK):
                    nc.tensor.matmul(
                        sum_bank[:, t, :],
                        lhsT=xi_planes[:, t, :],
                        rhs=ident[:],
                        start=True,
                        stop=False,
                        is_transpose=True,
                    )
                    nc.tensor.matmul(
                        sum_bank[:, t, :],
                        lhsT=xj_planes[:, t, :],
                        rhs=cross_perm[:, d, :, :].rearrange("k n i -> k (n i)"),
                        start=False,
                        stop=True,
                        is_transpose=True,
                    )
                nc.scalar.activation(
                    out=h_cross[g][:, d * ROWS * PACK : (d + 1) * ROWS * PACK].rearrange(
                        "p (r t) -> p r t", t=PACK
                    ),
                    in_=sum_bank[:].rearrange("p t r -> p r t"),
                    func=RELU,
                )

        def vector_line_adds(g):
            xi_t, xj_t = operands[g]
            receivers = xi_t[:].rearrange("p (h i) b t -> p h i b t", h=HALVES)
            shape = [P, HALVES, OTHERS, HALF, VECTOR_GRAPHS, PACK]
            nc.vector.tensor_tensor(
                out=h_same[g][:, FIRST_COLS * PACK : VECTOR_COLS * PACK].rearrange(
                    "p (h j i b t) -> p h j i b t", h=HALVES, j=OTHERS, i=HALF, t=PACK
                ),
                in0=receivers.unsqueeze(2).to_broadcast(shape),
                in1=xj_t[:, HALVES:, :, :]
                .rearrange("p (h j) b t -> p h j b t", h=HALVES)
                .unsqueeze(3)
                .to_broadcast(shape),
                op=ADD,
            )
            if not first_senders_are_plain(g):
                nc.vector.tensor_tensor(
                    out=h_same[g][:, 0 : FIRST_COLS * PACK].rearrange(
                        "p (h i b t) -> p h i b t", h=HALVES, i=HALF, t=PACK
                    ),
                    in0=receivers,
                    in1=xj_t[:, 0:HALVES, :, :]
                    .unsqueeze(2)
                    .to_broadcast([P, HALVES, HALF, VECTOR_GRAPHS, PACK]),
                    op=ADD,
                )

        def vector_relu(g):
            first = FIRST_COLS if first_senders_are_plain(g) else 0
            h_vector = h_same[g][:, first * PACK : VECTOR_COLS * PACK]
            nc.vector.tensor_scalar_max(out=h_vector, in0=h_vector, scalar1=0.0)

        def quantise(g, part):
            h = (h_cross, h_same)[part][g]
            h_codes = quantised.tile([P, PART_COLS], U32, align_bytes=64, tag="codes%d" % part)
            h_scales = quantised.tile([P, PART_COLS], U8, align_bytes=64, tag="scales%d" % part)
            mx_tiles[g, part] = (h_codes, h_scales)
            pieces = PART_BANKS if part == 0 and g == PASSES - 1 else 1
            width = PART_COLS // pieces
            for piece in range(pieces):
                cols = slice(piece * width, (piece + 1) * width)
                nc.vector.quantize_mx(
                    out=h_codes[:, cols].bitcast(FP8X4),
                    scales=h_scales[:, cols],
                    in_=h[:, piece * width * PACK : (piece + 1) * width * PACK],
                )

        def multiply(g):
            for q in BANK_ORDER:
                h_codes, h_scales = mx_tiles[g, q // PART_BANKS]
                cols = slice(q % PART_BANKS * BANK_COLS, (q % PART_BANKS + 1) * BANK_COLS)
                nc.tensor.matmul_mx(
                    out=acc[q][:],
                    lhsT=w_words[:, g, :].bitcast(FP8X4),
                    lhsT_scale=w_scales[:, g, :],
                    rhs=h_codes[:, cols].bitcast(FP8X4),
                    rhs_scale=h_scales[:, cols],
                    start=(g == 0),
                    stop=(g == PASSES - 1),
                )

        ident = const.tile([P, P], F32)
        make_identity(nc, ident[:])
        plain_rows = []
        first_rows = []
        for i in range(PLAIN_RING):
            for ring, name in ((plain_rows, "plain_rows%d"), (first_rows, "first_rows%d")):
                rows = const.tile([P, LOAD_COLS], BF16, name=name % i)
                engine = nc.vector if i == 0 and ring is plain_rows else nc.gpsimd
                engine.memset(rows[:].bitcast(I32), 0)
                ring.append(rows)
        load_rows(0, cuts=LOAD_PASSES)
        load_plain_rows(0)
        mb2_bf16 = const.tile([D_OUT, 1], BF16)
        nc.sync.dma_start(out=mb2_bf16[:], in_=mb2.rearrange("(d o) -> d o", o=1))
        mask_row = const.tile([P, GRAPHS, HALVES, HALF], BF16)
        nc.sync.dma_start(
            out=mask_row[:].rearrange("p b h i -> p (b h i)"),
            in_=node_mask.rearrange("b n -> (b n)").partition_broadcast(P),
        )
        w_words = const.tile([P, PASSES, PACK * D_OUT], U8, align_bytes=64)
        w_scales = const.tile([P, PASSES, D_OUT], U8, align_bytes=64)
        nc.gpsimd.memset(w_scales[:].rearrange("p g n -> p (g n)").bitcast(I32), 0)
        for quadrant in range(P // QUADRANT):
            first_row = quadrant * QUADRANT_SCALES
            first_partition = quadrant * QUADRANT
            nc.sync.dma_start(
                out=w_scales[first_partition : first_partition + QUADRANT_SCALES, :, :].bitcast(I32),
                in_=mw2_scales[:, first_row : first_row + QUADRANT_SCALES, :]
                .rearrange("g r n -> r g n")
                .bitcast(I32),
            )
        for g0 in range(0, PASSES, WEIGHT_LOAD_PASSES):
            nc.sync.dma_start(
                out=w_words[:, g0 : g0 + WEIGHT_LOAD_PASSES, :].bitcast(I32),
                in_=mw2_words[g0 : g0 + WEIGHT_LOAD_PASSES]
                .rearrange("g p n t -> p g (n t)")
                .bitcast(I32),
            )

        by_node = const.tile([P, P], F32)
        nc.vector.tensor_copy(
            out=by_node[:].rearrange("k (n b) -> k n b", b=GRAPHS),
            in_=ident[:].rearrange("k (b n) -> k n b", b=GRAPHS),
        )
        by_sender = const.tile([P, P], F32)
        nodes = by_node[:].rearrange("k (h j b) -> k h j b", h=HALVES, b=GRAPHS)
        first_end = HALVES * GRAPHS
        nc.vector.tensor_copy(
            out=by_sender[:, 0:first_end].rearrange("k (h b) -> k h b", h=HALVES),
            in_=nodes[:, :, 0, :],
        )
        nc.vector.tensor_copy(
            out=by_sender[:, first_end:].rearrange("k (h j b) -> k h j b", h=HALVES, b=GRAPHS),
            in_=nodes[:, :, 1:, :],
        )
        cross_perm = const.tile([ROWS, HALF, GRAPHS * HALVES, HALF], F32)
        swap_halves(
            nc.vector.tensor_copy,
            cross_perm[:, 0, :, :].rearrange("k (b h) i -> k b h i", h=HALVES),
            ident[:].rearrange("k (b h i) -> k b h i", h=HALVES, b=GRAPHS),
        )
        for d in range(1, HALF):
            rotate_in_halves(nc.vector.tensor_copy, cross_perm[:, d, :, :], cross_perm[:, 0, :, :], d)
        plain_select = const.tile([P, HALVES, HALF, HALF], BF16)

        first_select = const.tile([P, HALVES, HALF, VECTOR_GRAPHS], BF16)

        def build_plain_select():
            receivers = ident[:, 0:FIRST_XI_ROWS].rearrange("k (b h i) -> k h i b", h=HALVES, i=HALF)
            for half in range(HALVES):
                row = FIRST_XI_ROWS + half * VECTOR_GRAPHS
                nc.vector.scalar_tensor_tensor(
                    out=first_select[:, half, :, :],
                    in0=receivers[:, half, :, :],
                    scalar=ident[:, FIRST_MB1_ROW : FIRST_MB1_ROW + 1],
                    in1=ident[:, row : row + VECTOR_GRAPHS]
                    .unsqueeze(1)
                    .to_broadcast([P, HALF, VECTOR_GRAPHS]),
                    op0=ADD,
                    op1=ADD,
                )
            shape = [P, HALF, HALF]
            for half in range(HALVES):
                xi_first = half * HALF
                xj_first = PLAIN_XJ_ROW + half * HALF
                nc.vector.scalar_tensor_tensor(
                    out=plain_select[:, half, :, :],
                    in0=ident[:, xi_first : xi_first + HALF].unsqueeze(1).to_broadcast(shape),
                    scalar=ident[:, PLAIN_MB1_ROW : PLAIN_MB1_ROW + 1],
                    in1=ident[:, xj_first : xj_first + HALF].unsqueeze(2).to_broadcast(shape),
                    op0=ADD,
                    op1=ADD,
                )

        mb2_col = const.tile([D_OUT, 1], F32)
        nc.gpsimd.tensor_copy(out=mb2_col[:], in_=mb2_bf16[:])
        mask_cross = const.tile([P, HALF, GRAPHS * HALVES, HALF], F32)
        swap_halves(
            nc.gpsimd.tensor_copy,
            mask_cross[:, 0, :, :].rearrange("p (b h) i -> p b h i", h=HALVES),
            mask_row[:],
        )
        for d in range(1, HALF):
            rotate_in_halves(nc.gpsimd.tensor_copy, mask_cross[:, d, :, :], mask_cross[:, 0, :, :], d)
        mask_same = const.tile([P, HALVES, HALF, GRAPHS], F32)
        nc.gpsimd.tensor_copy(
            out=mask_same[:].rearrange("p h j b -> p (h j) b"),
            in_=mask_row[:].rearrange("p b h j -> p (h j) b"),
        )

        acc = [
            acc_banks.tile([D_OUT, BANK_COLS], F32, name="acc%d" % q) for q in range(2 * PART_BANKS)
        ]

        for r in range(-3, PASSES + 1):
            if 0 <= r + 1 < PASSES:
                h_same[r + 1] = hidden.tile([P, PART_COLS * PACK], BF16, align_bytes=64, name="same")
                h_cross[r + 1] = hidden.tile([P, PART_COLS * PACK], BF16, align_bytes=64, name="cross")
                vector_line_adds(r + 1)
            if 0 <= r and r + 1 < PASSES:
                plain_line(r + 1)
            if r >= 1:
                multiply(r - 1)
            if r + 3 < PASSES:
                sort_senders(r + 3)
            if r == -2:
                build_plain_select()
            if r < 0:
                sort_words(r + 3)
            if 0 <= r + 2 < PASSES:
                turn_operands(r + 2)
            if 0 <= r + 1 < PASSES:
                tensor_line(r + 1, 0, WORDS_PLACE)
            if 0 <= r and r + 3 < PASSES:
                sort_words(r + 3)
            if 0 <= r + 1 < PASSES:
                tensor_line(r + 1, WORDS_PLACE, HALF)
            if r == -1:
                plain_line(r + 1)
            if r + 3 < SORT_PASSES:
                sort_receivers(r + 3, 1)
            elif r + 3 < PASSES and (r + 3) % SORT_PASSES == 0:
                sort_receivers(r + 3, SORT_PASSES)
            if 0 <= r < PASSES:
                quantise(r, 1)
                quantise(r, 0)
            if 0 <= r + 1 < PASSES:
                vector_relu(r + 1)

        product = const.tile([D_OUT, 2 * PART_COLS], F32)
        msg = const.tile([D_OUT, NODES, GRAPHS, HALVES, HALF], F32)

        def finish_bank(q):
            nc.scalar.activation(
                out=product[:, q * BANK_COLS : (q + 1) * BANK_COLS],
                in_=acc[q][:],
                func=RELU,
                bias=mb2_col[:, 0:1],
            )

        for q in range(PART_BANKS, 2 * PART_BANKS):
            finish_bank(q)
        same = product[:, PART_COLS:]
        nc.vector.tensor_tensor(
            out=msg[:, HALF, 1:, :, :].rearrange("d b h i -> d h b i"),
            in0=same[:, 0:FIRST_COLS].rearrange("d (h i b) -> d h b i", h=HALVES, i=HALF),
            in1=mask_same[:, :, 0, 1:].unsqueeze(3).to_broadcast([D_OUT, HALVES, VECTOR_GRAPHS, HALF]),
            op=MULT,
        )
        for half in range(HALVES):
            col = FIRST_COLS + half * OTHERS * SENDER_COLS
            shape = [D_OUT, OTHERS, VECTOR_GRAPHS, HALF]
            nc.vector.tensor_tensor(
                out=msg[:, HALF + 1 : NODES, 1:, half, :],
                in0=same[:, col : col + OTHERS * SENDER_COLS].rearrange(
                    "d (j i b) -> d j b i", j=OTHERS, b=VECTOR_GRAPHS
                ),
                in1=mask_same[:, half, 1:, 1:].unsqueeze(3).to_broadcast(shape),
                op=MULT,
            )
            nc.vector.tensor_tensor(
                out=msg[:, HALF:NODES, 0, half, :],
                in0=same[:, VECTOR_COLS + half * HALF * HALF : VECTOR_COLS + (half + 1) * HALF * HALF]
                .rearrange("d (j i) -> d j i", j=HALF),
                in1=mask_same[:, half, :, 0:1].to_broadcast([D_OUT, HALF, HALF]),
                op=MULT,
            )
        for q in range(PART_BANKS):
            finish_bank(q)
            terms = slice(q * BANK_COLS // ROWS, (q + 1) * BANK_COLS // ROWS)
            nc.vector.tensor_tensor(
                out=msg[:, terms, :, :, :].rearrange("d m b h i -> d (m b h i)"),
                in0=product[:, q * BANK_COLS : (q + 1) * BANK_COLS],
                in1=mask_cross[:, terms, :, :].rearrange("d m n i -> d (m n i)"),
                op=MULT,
            )
        out_bank = work_banks.tile([ROWS, D_OUT], F32, tag="bank")
        for n in range(NODES):
            m = (HALF + n) % NODES
            nc.tensor.matmul(
                out_bank[:],
                lhsT=msg[:, m, :, :, :].rearrange("d b h i -> d (b h i)"),
                rhs=ident[:],
                start=(n == 0),
                stop=(n == NODES - 1),
                is_transpose=True,
            )
        out_sb = const.tile([ROWS, D_OUT], F32)
        nc.vector.tensor_copy(out=out_sb[:], in_=out_bank[:])
        nc.sync.dma_start(out=out_rows, in_=out_sb[:])
